import numpy as np
import ml_dtypes


def mxq(x, axis, fmt="e4m3"):
    dtype, down = {"e4m3": (ml_dtypes.float8_e4m3fn, 7), "e5m2": (ml_dtypes.float8_e5m2, 14)}[fmt]
    v = np.moveaxis(np.asarray(x, np.float32).astype(ml_dtypes.bfloat16).astype(np.float64), axis, -1)
    blocks = v.reshape(v.shape[:-1] + (-1, 32))
    amax = np.abs(blocks).max(-1, keepdims=True)
    byte = np.maximum(np.where(amax > 0, np.frexp(amax)[1] - 1 + 127, 0) - down, 1)
    scale = np.exp2(byte - 127.0)
    codes = (blocks / scale).astype(np.float32).astype(dtype).astype(np.float64)
    return np.moveaxis((codes * scale).reshape(v.shape), -1, axis)


WIDE = False


def mx_kscale(k):
    if not WIDE:
        return np.ones(k)
    levels = np.array([10, -10, 5, -5, 0])
    a = np.random.permutation(np.resize(levels, k // 512 * 4)).reshape(k // 512, 4)
    idx = np.arange(k)
    return np.exp2(a[idx // 512, idx % 128 // 32])


BF16 = ml_dtypes.bfloat16


def bf(x):
    return np.asarray(x, np.float32).astype(BF16)


def f64(x):
    return np.asarray(x).astype(np.float64)


B, S, HID, NH, DH, CHUNK = 1, 1536, 1024, 8, 128, 512
W = NH * DH
NC = S // CHUNK


def chunks(x):
    return x.reshape(B, S, NH, DH).transpose(0, 2, 1, 3).reshape(B, NH, NC, CHUNK, DH)


def with_prev(own, prev, op):
    return np.concatenate([own[:, :, :1], op(own[:, :, 1:], prev)], axis=2)


def setup_inputs():
    s = mx_kscale(HID)
    return {"q": bf(np.random.standard_normal((B, S, W)) * np.sqrt(2.0)),
            "k_scaled": bf(np.random.standard_normal((B, S, W)) * np.sqrt(2.0 / DH)),
            "hidden_states": bf(np.random.standard_normal((B, S, HID)) * s),
            "Wv": bf(np.random.standard_normal((HID, W)) / np.sqrt(HID) / s[:, None])}


def reference(q, k_scaled, hidden_states, Wv):
    q5, k5 = chunks(f64(q)), chunks(f64(k_scaled))
    v = mxq(f64(hidden_states), 2, "e4m3") @ mxq(f64(Wv), 0, "e4m3")
    vq = mxq(chunks(v), 3, "e4m3")
    pos = np.arange(CHUNK)
    later = np.where(pos[:, None] < pos[None, :], 1e9, 0.0)
    d_own = q5 @ k5.transpose(0, 1, 2, 4, 3) - later
    d_prev = q5[:, :, 1:] @ k5[:, :, :-1].transpose(0, 1, 2, 4, 3)
    m = with_prev(d_own.max(-1, keepdims=True), d_prev.max(-1, keepdims=True), np.maximum)
    e_own = np.exp(d_own - m)
    e_prev = np.exp(d_prev - m[:, :, 1:])
    den = with_prev(e_own.sum(-1, keepdims=True), e_prev.sum(-1, keepdims=True), np.add)
    num = with_prev(mxq(e_own, 4, "e4m3") @ vq, mxq(e_prev, 4, "e4m3") @ vq[:, :, :-1], np.add)
    res = num / den
    return res.reshape(B, NH, S, DH).transpose(0, 2, 1, 3).reshape(B, S, W)

@@ -1,0 +1,348 @@
+from contextlib import ExitStack
+
+import concourse.mybir as mybir
+from concourse.masks import make_identity
+
+BF16 = mybir.dt.bfloat16
+F32 = mybir.dt.float32
+U32 = mybir.dt.uint32
+U8 = mybir.dt.uint8
+FP8X4 = mybir.dt.float8_e4m3fn_x4
+ALU = mybir.AluOpType
+ACT = mybir.ActivationFunctionType
+AX = mybir.AxisListType
+
+P = 128
+PACK = 4
+K_PASS = P * PACK
+
+SEQ, HID, HEADS, DH, CHUNK = 1536, 1024, 8, 128, 512
+WIDTH = HEADS * DH
+HALF = WIDTH // 2
+CHUNKS = SEQ // CHUNK
+QTILES = CHUNK // P
+HID_PASSES = HID // K_PASS
+PREV, OWN = 0, 1
+MASKED = -1.0e9
+
+FLOPS = 2 * SEQ * HID * WIDTH + 2 * 2 * HEADS * (2 * CHUNKS - 1) * CHUNK * CHUNK * DH
+
+
+def tile_localselfattention_pa_kernel(tc, q, k_scaled, hidden_states, Wv, out):
+    nc = tc.nc
+    with ExitStack() as ctx:
+        const = ctx.enter_context(tc.tile_pool(name="const", bufs=1))
+        raw = ctx.enter_context(tc.tile_pool(name="raw", bufs=2))
+        keep = ctx.enter_context(tc.tile_pool(name="keep", bufs=1))
+        work = ctx.enter_context(tc.tile_pool(name="work", bufs=3))
+        small = ctx.enter_context(tc.tile_pool(name="small", bufs=6))
+        ps_scores = ctx.enter_context(tc.psum_pool(name="ps_scores", bufs=2))
+        ps_et = ctx.enter_context(tc.psum_pool(name="ps_et", bufs=2))
+        ps_o = ctx.enter_context(tc.psum_pool(name="ps_o", bufs=1))
+        ps_prep = ctx.enter_context(tc.psum_pool(name="ps_prep", bufs=1))
+
+        ident_bf = const.tile([P, P], BF16, name="ident_bf")
+        make_identity(nc, ident_bf[:])
+        ident_f32 = const.tile([P, P], F32, name="ident_f32")
+        make_identity(nc, ident_f32[:])
+        mask_f32 = const.tile([P, P], F32, name="mask_f32")
+        nc.gpsimd.memset(mask_f32[:], 0.0)
+        nc.gpsimd.affine_select(
+            out=mask_f32[:],
+            in_=mask_f32[:],
+            compare_op=ALU.is_ge,
+            fill=MASKED,
+            base=0,
+            pattern=[[-1, P]],
+            channel_multiplier=1,
+        )
+        mask_bf = const.tile([P, P], BF16, name="mask_bf")
+        nc.vector.tensor_copy(out=mask_bf[:], in_=mask_f32[:])
+
+        e_tiles = []
+        for i in range(QTILES):
+            e_tile = keep.tile([P, 2 * CHUNK], BF16, name="e_tile%d" % i)
+            if (i + 1) * P < CHUNK:
+                nc.vector.memset(e_tile[:, OWN * CHUNK + (i + 1) * P :], 0.0)
+            e_tiles.append(e_tile)
+
+        wv_raw = keep.tile([P, HID_PASSES, PACK, WIDTH], BF16, name="wv_raw")
+        wv_codes = keep.tile([P, HID_PASSES, WIDTH], U32, name="wv_codes", align_bytes=64)
+        wv_scales = keep.tile([P, HID_PASSES, WIDTH], U8, name="wv_scales", align_bytes=64)
+        hid_codes = keep.tile([P, CHUNKS, QTILES, HID_PASSES * P], U32, name="hid_codes", align_bytes=64)
+        hid_scales = keep.tile([P, CHUNKS, QTILES, HID_PASSES * P], U8, name="hid_scales", align_bytes=64)
+        v_codes = keep.tile([P, CHUNKS, HEADS, DH], U32, name="v_codes", align_bytes=64)
+        v_scales = keep.tile([P, CHUNKS, HEADS, DH], U8, name="v_scales", align_bytes=64)
+        qk_t = keep.tile([P, CHUNKS, HEADS, 2, CHUNK], BF16, name="qk_t")
+
+        raw_tiles = {}
+
+        def load_wv(g, half):
+            cols = slice(half * HALF, (half + 1) * HALF)
+            for u in range(2):
+                first = g * K_PASS + u * 2 * P
+                nc.sync.dma_start(
+                    out=wv_raw[:, g, 2 * u : 2 * u + 2, cols],
+                    in_=Wv[first : first + 2 * P, cols].rearrange("(p e) n -> p e n", e=2),
+                )
+
+        def load_hidden(n):
+            rows = slice(n * CHUNK, (n + 1) * CHUNK)
+            hid_raw = raw.tile([P, QTILES * HID], BF16, name="hid_raw", tag="hid_raw")
+            nc.sync.dma_start(
+                out=hid_raw[:].rearrange("p (u ew) -> p u ew", u=2),
+                in_=hidden_states[0, rows, :].rearrange("(u p e) w -> p u (e w)", u=2, p=P, e=2),
+            )
+            raw_tiles[("hid", n)] = hid_raw
+
+        def load_qk(n, half):
+            rows = slice(n * CHUNK, (n + 1) * CHUNK)
+            cols = slice(half * HALF, (half + 1) * HALF)
+            if half == 0:
+                q_raw = raw.tile([P, QTILES, WIDTH], BF16, name="q_raw", tag="q_raw")
+                k_raw = raw.tile([P, QTILES, WIDTH], BF16, name="k_raw", tag="k_raw")
+                raw_tiles[("q", n)] = q_raw
+                raw_tiles[("k", n)] = k_raw
+            nc.sync.dma_start(out=raw_tiles[("q", n)][:, :, cols], in_=q[0, rows, cols].rearrange("(r p) w -> p r w", p=P))
+            nc.sync.dma_start(out=raw_tiles[("k", n)][:, :, cols], in_=k_scaled[0, rows, cols].rearrange("(r p) w -> p r w", p=P))
+
+        def prep_wv(g, half):
+            cols = slice(half * HALF, (half + 1) * HALF)
+            wv_grouped = work.tile([P, HALF, PACK], BF16, name="wv_grouped", tag="wv_grouped", align_bytes=64)
+            nc.vector.tensor_copy(
+                out=wv_grouped[:].rearrange("p (c i) t -> p c t i", i=4),
+                in_=wv_raw[:, g, :, cols].rearrange("p t (c i) -> p c t i", i=4),
+            )
+            nc.vector.quantize_mx(
+                out=wv_codes[:, g, cols].bitcast(FP8X4),
+                scales=wv_scales[:, g, cols],
+                in_=wv_grouped[:].rearrange("p n t -> p (n t)"),
+            )
+
+        def prep_hidden(n, t):
+            words = raw_tiles[("hid", n)][:].bitcast(F32)
+            hid_t = ps_prep.tile([P, PACK, P], F32, name="hid_t", tag="prep")
+            for gu in range(PACK):
+                first = t * (HID // 2) + gu * P
+                nc.tensor.transpose(out=hid_t[:, gu, :], in_=words[:, first : first + P], identity=ident_f32[:])
+            hid_grouped = work.tile([P, HID_PASSES * P * PACK], BF16, name="hid_grouped", tag="hid_grouped", align_bytes=64)
+            nc.scalar.copy(
+                out=hid_grouped[:].bitcast(F32).rearrange("p (g r u) -> p g r u", g=HID_PASSES, u=2),
+                in_=hid_t[:].rearrange("p (g u) r -> p g r u", g=HID_PASSES),
+            )
+            nc.vector.quantize_mx(
+                out=hid_codes[:, n, t, :].bitcast(FP8X4),
+                scales=hid_scales[:, n, t, :],
+                in_=hid_grouped[:],
+            )
+
+        def prep_qk(n, h):
+            cols = slice(h * DH, (h + 1) * DH)
+            qk_ps = ps_prep.tile([P, 2, CHUNK], BF16, name="qk_ps", tag="prep")
+            for which, key in enumerate(("q", "k")):
+                src = raw_tiles[(key, n)]
+                for r in range(QTILES):
+                    nc.tensor.transpose(out=qk_ps[:, which, r * P : (r + 1) * P], in_=src[:, r, cols], identity=ident_bf[:])
+            nc.vector.tensor_copy(out=qk_t[:, n, h], in_=qk_ps[:])
+
+        def prep_v(n, h):
+            cols = slice(h * DH, (h + 1) * DH)
+            v_ps = ps_prep.tile([P, PACK, DH], F32, name="v_ps", tag="prep")
+            for t in range(PACK):
+                for g in range(HID_PASSES):
+                    nc.tensor.matmul_mx(
+                        out=v_ps[:, t, :],
+                        lhsT=hid_codes[:, n, t, g * P : (g + 1) * P].bitcast(FP8X4),
+                        lhsT_scale=hid_scales[:, n, t, g * P : (g + 1) * P],
+                        rhs=wv_codes[:, g, cols].bitcast(FP8X4),
+                        rhs_scale=wv_scales[:, g, cols],
+                        start=(g == 0),
+                        stop=(g == HID_PASSES - 1),
+                    )
+            v_grouped = work.tile([P, DH, PACK], BF16, name="v_grouped", tag="v_grouped", align_bytes=64)
+            nc.scalar.copy(out=v_grouped[:], in_=v_ps[:].rearrange("p t d -> p d t"))
+            nc.vector.quantize_mx(
+                out=v_codes[:, n, h, :].bitcast(FP8X4),
+                scales=v_scales[:, n, h, :],
+                in_=v_grouped[:].rearrange("p d t -> p (d t)"),
+            )
+
+        groups = [(n, h) for n in range(CHUNKS) for h in range(HEADS)]
+        units = [(n, h, i) for (n, h) in groups for i in range(QTILES)]
+        live = {}
+
+        def scores(u):
+            n, h, i = units[u]
+            q_cols = qk_t[:, n, h, 0, i * P : (i + 1) * P]
+            banks = {}
+            if n > 0:
+                s_prev = ps_scores.tile([P, CHUNK], F32, name="s_prev", tag="s_prev")
+                nc.tensor.matmul(out=s_prev[:], lhsT=q_cols, rhs=qk_t[:, n - 1, h, 1, :], start=True, stop=True)
+                banks[PREV] = s_prev
+            s_own = ps_scores.tile([P, CHUNK], F32, name="s_own", tag="s_own")
+            if i > 0:
+                nc.tensor.matmul(out=s_own[:, : i * P], lhsT=q_cols, rhs=qk_t[:, n, h, 1, : i * P], start=True, stop=True)
+            diag = slice(i * P, (i + 1) * P)
+            nc.tensor.matmul(out=s_own[:, diag], lhsT=ident_bf[:], rhs=mask_bf[:], start=True, stop=False)
+            nc.tensor.matmul(out=s_own[:, diag], lhsT=q_cols, rhs=qk_t[:, n, h, 1, diag], start=False, stop=True)
+            banks[OWN] = s_own
+            live[("scores", u)] = banks
+
+        def widths(u):
+            n, h, i = units[u]
+            return {PREV: CHUNK, OWN: (i + 1) * P}
+
+        def sides(u):
+            return (OWN,) if units[u][0] == 0 else (PREV, OWN)
+
+        def row_max(u):
+            banks = live[("scores", u)]
+            parts = small.tile([P, 2], F32, name="negmax_parts", tag="negmax_parts")
+            for a in sides(u):
+                nc.vector.tensor_reduce(
+                    out=parts[:, a : a + 1], in_=banks[a][:, : widths(u)[a]], axis=AX.X, op=ALU.max, negate=True
+                )
+            if len(sides(u)) == 2:
+                negmax = small.tile([P, 1], F32, name="negmax", tag="negmax")
+                nc.vector.tensor_tensor(out=negmax[:], in0=parts[:, PREV : PREV + 1], in1=parts[:, OWN : OWN + 1], op=ALU.min)
+                live[("negmax", u)] = negmax[:]
+            else:
+                live[("negmax", u)] = parts[:, OWN : OWN + 1]
+
+        def exponentials(u):
+            n, h, i = units[u]
+            banks = live[("scores", u)]
+            if i == 0:
+                sums = small.tile([P, QTILES, 2], F32, name="sums", tag="sums")
+                live[("sums", n, h)] = sums
+            sums = live[("sums", n, h)]
+            for a in sides(u):
+                w = widths(u)[a]
+                nc.scalar.activation(
+                    out=e_tiles[i][:, a * CHUNK : a * CHUNK + w],
+                    in_=banks[a][:, :w],
+                    func=ACT.Exp,
+                    bias=live[("negmax", u)],
+                    scale=1.0,
+                    accum_out=sums[:, i, a : a + 1],
+                )
+
+        def transposes(u):
+            n, h, i = units[u]
+            e_t = ps_et.tile([P, 2, 2, P], F32, name="e_t", tag="e_t")
+            words = e_tiles[i][:].bitcast(F32)
+            for a in sides(u):
+                for half in range(2):
+                    first = (2 * a + half) * P
+                    nc.tensor.transpose(out=e_t[:, a, half, :], in_=words[:, first : first + P], identity=ident_f32[:])
+            live[("e_t", u)] = e_t
+
+        def regroup(u):
+            first = sides(u)[0]
+            e_grouped = work.tile([P, 2 * P * PACK], BF16, name="e_grouped", tag="e_grouped", align_bytes=64)
+            nc.scalar.copy(
+                out=e_grouped[:].bitcast(F32).rearrange("p (a r half) -> p a r half", a=2, half=2)[:, first:],
+                in_=live[("e_t", u)][:, first:].rearrange("p a half r -> p a r half"),
+            )
+            live[("e_grouped", u)] = e_grouped
+
+        def quantise(u):
+            first = sides(u)[0]
+            e_codes = work.tile([P, 2, P], U32, name="e_codes", tag="e_codes", align_bytes=64)
+            e_scales = work.tile([P, 2, P], U8, name="e_scales", tag="e_scales", align_bytes=64)
+            nc.vector.quantize_mx(
+                out=e_codes[:, first:].rearrange("p a r -> p (a r)").bitcast(FP8X4),
+                scales=e_scales[:, first:].rearrange("p a r -> p (a r)"),
+                in_=live[("e_grouped", u)][:, first * P * PACK :],
+            )
+            live[("e_codes", u)] = (e_codes, e_scales)
+
+        def multiply(u):
+            n, h, i = units[u]
+            if i == 0:
+                o_ps = ps_o.tile([P, QTILES, DH], F32, name="o_ps", tag="o_ps")
+                live[("o_ps", n, h)] = o_ps
+            o_ps = live[("o_ps", n, h)]
+            e_codes, e_scales = live[("e_codes", u)]
+            for a in sides(u):
+                nc.tensor.matmul_mx(
+                    out=o_ps[:, i, :],
+                    lhsT=e_codes[:, a, :].bitcast(FP8X4),
+                    lhsT_scale=e_scales[:, a, :],
+                    rhs=v_codes[:, n - 1 + a, h, :].bitcast(FP8X4),
+                    rhs_scale=v_scales[:, n - 1 + a, h, :],
+                    start=(a == sides(u)[0]),
+                    stop=(a == OWN),
+                )
+
+        def finish(n, h):
+            sums = live[("sums", n, h)]
+            recip = small.tile([P, QTILES], F32, name="recip", tag="recip")
+            if n == 0:
+                nc.vector.reciprocal(out=recip[:], in_=sums[:, :, OWN])
+            else:
+                den = small.tile([P, QTILES], F32, name="den", tag="den")
+                nc.vector.tensor_tensor(out=den[:], in0=sums[:, :, PREV], in1=sums[:, :, OWN], op=ALU.add)
+                nc.vector.reciprocal(out=recip[:], in_=den[:])
+            o_sb = work.tile([P, QTILES, DH], F32, name="o_sb", tag="o_sb")
+            nc.vector.tensor_tensor(
+                out=o_sb[:],
+                in0=live[("o_ps", n, h)][:],
+                in1=recip[:].unsqueeze(2).to_broadcast([P, QTILES, DH]),
+                op=ALU.mult,
+            )
+            nc.sync.dma_start(
+                out=out[0, n * CHUNK : (n + 1) * CHUNK, h * DH : (h + 1) * DH].rearrange("(i p) d -> p i d", p=P),
+                in_=o_sb[:],
+            )
+
+        load_wv(0, 0)
+        load_wv(1, 0)
+        load_hidden(0)
+        load_qk(0, 0)
+        load_wv(0, 1)
+        load_wv(1, 1)
+        load_qk(0, 1)
+        load_hidden(1)
+        load_qk(1, 0)
+        load_qk(1, 1)
+
+        for g in range(HID_PASSES):
+            prep_wv(g, 0)
+        for t in range(QTILES):
+            prep_hidden(0, t)
+        prep_v(0, 0)
+        prep_qk(0, 0)
+
+        count = len(units)
+        for step in range(count + 4):
+            if step < count:
+                n, h, i = units[step]
+                scores(step)
+                row_max(step)
+                nxt = step // QTILES + 1
+                if i == 0 and n == 1 and h == 0:
+                    load_hidden(2)
+                    load_qk(2, 0)
+                    load_qk(2, 1)
+                if i == 0 and nxt < len(groups):
+                    prep_qk(*groups[nxt])
+                if i == 1 and h < QTILES and n + 1 < CHUNKS:
+                    prep_hidden(n + 1, h)
+                if i == 2 and nxt < len(groups):
+                    prep_v(*groups[nxt])
+                if i == 3 and n == 0 and h < HID_PASSES:
+                    prep_wv(h, 1)
+            if 0 <= step - 3 < count:
+                regroup(step - 3)
+            if 0 <= step - 1 < count:
+                exponentials(step - 1)
+            if 0 <= step - 2 < count:
+                transposes(step - 2)
+            if 0 <= step - 3 < count:
+                quantise(step - 3)
+            if 0 <= step - 4 < count:
+                multiply(step - 4)
+                n, h, i = units[step - 4]
+                if i == QTILES - 1:
+                    finish(n, h)

@@ -76,6 +76,7 @@ def tile_localselfattention_pa_kernel(tc, q, k_scaled, hidden_states, Wv, out):
         qk_t = keep.tile([P, CHUNKS, HEADS, 2, CHUNK], BF16, name="qk_t")
 
         raw_tiles = {}
+        live = {}
 
         def load_wv(g, half):
             cols = slice(half * HALF, (half + 1) * HALF)
@@ -106,7 +107,7 @@ def tile_localselfattention_pa_kernel(tc, q, k_scaled, hidden_states, Wv, out):
             nc.sync.dma_start(out=raw_tiles[("q", n)][:, :, cols], in_=q[0, rows, cols].rearrange("(r p) w -> p r w", p=P))
             nc.sync.dma_start(out=raw_tiles[("k", n)][:, :, cols], in_=k_scaled[0, rows, cols].rearrange("(r p) w -> p r w", p=P))
 
-        def prep_wv(g, half):
+        def wv_quantise(g, half):
             cols = slice(half * HALF, (half + 1) * HALF)
             wv_grouped = work.tile([P, HALF, PACK], BF16, name="wv_grouped", tag="wv_grouped", align_bytes=64)
             nc.vector.tensor_copy(
@@ -119,33 +120,42 @@ def tile_localselfattention_pa_kernel(tc, q, k_scaled, hidden_states, Wv, out):
                 in_=wv_grouped[:].rearrange("p n t -> p (n t)"),
             )
 
-        def prep_hidden(n, t):
+        def hidden_transposes(n, t, pool, tag):
             words = raw_tiles[("hid", n)][:].bitcast(F32)
-            hid_t = ps_prep.tile([P, PACK, P], F32, name="hid_t", tag="prep")
+            hid_t = pool.tile([P, PACK, P], F32, name="hid_t", tag=tag)
             for gu in range(PACK):
                 first = t * (HID // 2) + gu * P
                 nc.tensor.transpose(out=hid_t[:, gu, :], in_=words[:, first : first + P], identity=ident_f32[:])
+            live[("hid_t", n, t)] = hid_t
+
+        def hidden_copy(n, t):
             hid_grouped = work.tile([P, HID_PASSES * P * PACK], BF16, name="hid_grouped", tag="hid_grouped", align_bytes=64)
             nc.scalar.copy(
                 out=hid_grouped[:].bitcast(F32).rearrange("p (g r u) -> p g r u", g=HID_PASSES, u=2),
-                in_=hid_t[:].rearrange("p (g u) r -> p g r u", g=HID_PASSES),
+                in_=live[("hid_t", n, t)][:].rearrange("p (g u) r -> p g r u", g=HID_PASSES),
             )
+            live[("hid_grouped", n, t)] = hid_grouped
+
+        def hidden_quantise(n, t):
             nc.vector.quantize_mx(
                 out=hid_codes[:, n, t, :].bitcast(FP8X4),
                 scales=hid_scales[:, n, t, :],
-                in_=hid_grouped[:],
+                in_=live[("hid_grouped", n, t)][:],
             )
 
-        def prep_qk(n, h):
+        def qk_transposes(n, h):
             cols = slice(h * DH, (h + 1) * DH)
             qk_ps = ps_prep.tile([P, 2, CHUNK], BF16, name="qk_ps", tag="prep")
             for which, key in enumerate(("q", "k")):
                 src = raw_tiles[(key, n)]
                 for r in range(QTILES):
                     nc.tensor.transpose(out=qk_ps[:, which, r * P : (r + 1) * P], in_=src[:, r, cols], identity=ident_bf[:])
-            nc.vector.tensor_copy(out=qk_t[:, n, h], in_=qk_ps[:])
+            live[("qk_ps", n, h)] = qk_ps
 
-        def prep_v(n, h):
+        def qk_copy(n, h):
+            nc.vector.tensor_copy(out=qk_t[:, n, h], in_=live[("qk_ps", n, h)][:])
+
+        def v_project(n, h):
             cols = slice(h * DH, (h + 1) * DH)
             v_ps = ps_prep.tile([P, PACK, DH], F32, name="v_ps", tag="prep")
             for t in range(PACK):
@@ -159,17 +169,22 @@ def tile_localselfattention_pa_kernel(tc, q, k_scaled, hidden_states, Wv, out):
                         start=(g == 0),
                         stop=(g == HID_PASSES - 1),
                     )
+            live[("v_ps", n, h)] = v_ps
+
+        def v_copy(n, h):
             v_grouped = work.tile([P, DH, PACK], BF16, name="v_grouped", tag="v_grouped", align_bytes=64)
-            nc.scalar.copy(out=v_grouped[:], in_=v_ps[:].rearrange("p t d -> p d t"))
+            nc.scalar.copy(out=v_grouped[:], in_=live[("v_ps", n, h)][:].rearrange("p t d -> p d t"))
+            live[("v_grouped", n, h)] = v_grouped
+
+        def v_quantise(n, h):
             nc.vector.quantize_mx(
                 out=v_codes[:, n, h, :].bitcast(FP8X4),
                 scales=v_scales[:, n, h, :],
-                in_=v_grouped[:].rearrange("p d t -> p (d t)"),
+                in_=live[("v_grouped", n, h)][:].rearrange("p d t -> p (d t)"),
             )
 
         groups = [(n, h) for n in range(CHUNKS) for h in range(HEADS)]
         units = [(n, h, i) for (n, h) in groups for i in range(QTILES)]
-        live = {}
 
         def scores(u):
             n, h, i = units[u]
@@ -296,6 +311,7 @@ def tile_localselfattention_pa_kernel(tc, q, k_scaled, hidden_states, Wv, out):
                 in_=o_sb[:],
             )
 
+        ctx.enter_context(tc.manual_schedule())
         load_wv(0, 0)
         load_wv(1, 0)
         load_hidden(0)
@@ -308,41 +324,56 @@ def tile_localselfattention_pa_kernel(tc, q, k_scaled, hidden_states, Wv, out):
         load_qk(1, 1)
 
         for g in range(HID_PASSES):
-            prep_wv(g, 0)
+            wv_quantise(g, 0)
         for t in range(QTILES):
-            prep_hidden(0, t)
-        prep_v(0, 0)
-        prep_qk(0, 0)
+            hidden_transposes(0, t, ps_et, "e_t")
+            hidden_copy(0, t)
+            hidden_quantise(0, t)
+        v_project(0, 0)
+        v_copy(0, 0)
+        v_quantise(0, 0)
+        qk_transposes(0, 0)
+        qk_copy(0, 0)
 
         count = len(units)
         for step in range(count + 4):
-            if step < count:
+            front = step < count
+            if front:
                 n, h, i = units[step]
-                scores(step)
-                row_max(step)
                 nxt = step // QTILES + 1
+                more = nxt < len(groups)
+                hidden_next = h < QTILES and n + 1 < CHUNKS
                 if i == 0 and n == 1 and h == 0:
                     load_hidden(2)
                     load_qk(2, 0)
                     load_qk(2, 1)
-                if i == 0 and nxt < len(groups):
-                    prep_qk(*groups[nxt])
-                if i == 1 and h < QTILES and n + 1 < CHUNKS:
-                    prep_hidden(n + 1, h)
-                if i == 2 and nxt < len(groups):
-                    prep_v(*groups[nxt])
-                if i == 3 and n == 0 and h < HID_PASSES:
-                    prep_wv(h, 1)
+                scores(step)
+            if 0 <= step - 4 < count:
+                quantise(step - 4)
             if 0 <= step - 3 < count:
                 regroup(step - 3)
             if 0 <= step - 1 < count:
                 exponentials(step - 1)
+            if front and i == 0 and more:
+                qk_transposes(*groups[nxt])
+                qk_copy(*groups[nxt])
+            if front and i == 1 and hidden_next:
+                hidden_transposes(n + 1, h, ps_prep, "prep")
+                hidden_copy(n + 1, h)
             if 0 <= step - 2 < count:
                 transposes(step - 2)
-            if 0 <= step - 3 < count:
-                quantise(step - 3)
+            if front and i == 2 and more:
+                v_project(*groups[nxt])
+                v_copy(*groups[nxt])
             if 0 <= step - 4 < count:
                 multiply(step - 4)
-                n, h, i = units[step - 4]
-                if i == QTILES - 1:
-                    finish(n, h)
+            if front and i == 2 and hidden_next:
+                hidden_quantise(n + 1, h)
+            if front and i == 3 and more:
+                v_quantise(*groups[nxt])
+            if front and i == 3 and n == 0 and h < HID_PASSES:
+                wv_quantise(h, 1)
+            if front:
+                row_max(step)
+            if 0 <= step - 4 < count and units[step - 4][2] == QTILES - 1:
+                finish(units[step - 4][0], units[step - 4][1])

@@ -36,6 +36,7 @@ def tile_localselfattention_pa_kernel(tc, q, k_scaled, hidden_states, Wv, out):
         keep = ctx.enter_context(tc.tile_pool(name="keep", bufs=1))
         work = ctx.enter_context(tc.tile_pool(name="work", bufs=3))
         small = ctx.enter_context(tc.tile_pool(name="small", bufs=6))
+        ahead = ctx.enter_context(tc.tile_pool(name="ahead", bufs=3))
         ps_scores = ctx.enter_context(tc.psum_pool(name="ps_scores", bufs=2))
         ps_et = ctx.enter_context(tc.psum_pool(name="ps_et", bufs=2))
         ps_o = ctx.enter_context(tc.psum_pool(name="ps_o", bufs=1))
@@ -76,7 +77,6 @@ def tile_localselfattention_pa_kernel(tc, q, k_scaled, hidden_states, Wv, out):
         qk_t = keep.tile([P, CHUNKS, HEADS, 2, CHUNK], BF16, name="qk_t")
 
         raw_tiles = {}
-        live = {}
 
         def load_wv(g, half):
             cols = slice(half * HALF, (half + 1) * HALF)
@@ -107,7 +107,7 @@ def tile_localselfattention_pa_kernel(tc, q, k_scaled, hidden_states, Wv, out):
             nc.sync.dma_start(out=raw_tiles[("q", n)][:, :, cols], in_=q[0, rows, cols].rearrange("(r p) w -> p r w", p=P))
             nc.sync.dma_start(out=raw_tiles[("k", n)][:, :, cols], in_=k_scaled[0, rows, cols].rearrange("(r p) w -> p r w", p=P))
 
-        def wv_quantise(g, half):
+        def prep_wv(g, half):
             cols = slice(half * HALF, (half + 1) * HALF)
             wv_grouped = work.tile([P, HALF, PACK], BF16, name="wv_grouped", tag="wv_grouped", align_bytes=64)
             nc.vector.tensor_copy(
@@ -120,42 +120,33 @@ def tile_localselfattention_pa_kernel(tc, q, k_scaled, hidden_states, Wv, out):
                 in_=wv_grouped[:].rearrange("p n t -> p (n t)"),
             )
 
-        def hidden_transposes(n, t, pool, tag):
+        def prep_hidden(n, t):
             words = raw_tiles[("hid", n)][:].bitcast(F32)
-            hid_t = pool.tile([P, PACK, P], F32, name="hid_t", tag=tag)
+            hid_t = ps_prep.tile([P, PACK, P], F32, name="hid_t", tag="prep")
             for gu in range(PACK):
                 first = t * (HID // 2) + gu * P
                 nc.tensor.transpose(out=hid_t[:, gu, :], in_=words[:, first : first + P], identity=ident_f32[:])
-            live[("hid_t", n, t)] = hid_t
-
-        def hidden_copy(n, t):
             hid_grouped = work.tile([P, HID_PASSES * P * PACK], BF16, name="hid_grouped", tag="hid_grouped", align_bytes=64)
             nc.scalar.copy(
                 out=hid_grouped[:].bitcast(F32).rearrange("p (g r u) -> p g r u", g=HID_PASSES, u=2),
-                in_=live[("hid_t", n, t)][:].rearrange("p (g u) r -> p g r u", g=HID_PASSES),
+                in_=hid_t[:].rearrange("p (g u) r -> p g r u", g=HID_PASSES),
             )
-            live[("hid_grouped", n, t)] = hid_grouped
-
-        def hidden_quantise(n, t):
             nc.vector.quantize_mx(
                 out=hid_codes[:, n, t, :].bitcast(FP8X4),
                 scales=hid_scales[:, n, t, :],
-                in_=live[("hid_grouped", n, t)][:],
+                in_=hid_grouped[:],
             )
 
-        def qk_transposes(n, h):
+        def prep_qk(n, h):
             cols = slice(h * DH, (h + 1) * DH)
             qk_ps = ps_prep.tile([P, 2, CHUNK], BF16, name="qk_ps", tag="prep")
             for which, key in enumerate(("q", "k")):
                 src = raw_tiles[(key, n)]
                 for r in range(QTILES):
                     nc.tensor.transpose(out=qk_ps[:, which, r * P : (r + 1) * P], in_=src[:, r, cols], identity=ident_bf[:])
-            live[("qk_ps", n, h)] = qk_ps
+            nc.vector.tensor_copy(out=qk_t[:, n, h], in_=qk_ps[:])
 
-        def qk_copy(n, h):
-            nc.vector.tensor_copy(out=qk_t[:, n, h], in_=live[("qk_ps", n, h)][:])
-
-        def v_project(n, h):
+        def prep_v(n, h):
             cols = slice(h * DH, (h + 1) * DH)
             v_ps = ps_prep.tile([P, PACK, DH], F32, name="v_ps", tag="prep")
             for t in range(PACK):
@@ -169,22 +160,17 @@ def tile_localselfattention_pa_kernel(tc, q, k_scaled, hidden_states, Wv, out):
                         start=(g == 0),
                         stop=(g == HID_PASSES - 1),
                     )
-            live[("v_ps", n, h)] = v_ps
-
-        def v_copy(n, h):
             v_grouped = work.tile([P, DH, PACK], BF16, name="v_grouped", tag="v_grouped", align_bytes=64)
-            nc.scalar.copy(out=v_grouped[:], in_=live[("v_ps", n, h)][:].rearrange("p t d -> p d t"))
-            live[("v_grouped", n, h)] = v_grouped
-
-        def v_quantise(n, h):
+            nc.scalar.copy(out=v_grouped[:], in_=v_ps[:].rearrange("p t d -> p d t"))
             nc.vector.quantize_mx(
                 out=v_codes[:, n, h, :].bitcast(FP8X4),
                 scales=v_scales[:, n, h, :],
-                in_=live[("v_grouped", n, h)][:].rearrange("p d t -> p (d t)"),
+                in_=v_grouped[:].rearrange("p d t -> p (d t)"),
             )
 
         groups = [(n, h) for n in range(CHUNKS) for h in range(HEADS)]
         units = [(n, h, i) for (n, h) in groups for i in range(QTILES)]
+        live = {}
 
         def scores(u):
             n, h, i = units[u]
@@ -212,35 +198,39 @@ def tile_localselfattention_pa_kernel(tc, q, k_scaled, hidden_states, Wv, out):
 
         def row_max(u):
             banks = live[("scores", u)]
-            parts = small.tile([P, 2], F32, name="negmax_parts", tag="negmax_parts")
+            neg_s = ahead.tile([P, 2 * CHUNK], F32, name="neg_s", tag="neg_s")
+            running = None
             for a in sides(u):
-                nc.vector.tensor_reduce(
-                    out=parts[:, a : a + 1], in_=banks[a][:, : widths(u)[a]], axis=AX.X, op=ALU.max, negate=True
+                w = widths(u)[a]
+                negmax = small.tile([P, 1], F32, name="negmax%d" % a, tag="negmax%d" % a)
+                nc.vector.tensor_scalar(
+                    out=neg_s[:, a * CHUNK : a * CHUNK + w],
+                    in0=banks[a][:, :w],
+                    scalar1=-1.0,
+                    scalar2=running,
+                    op0=ALU.mult,
+                    op1=ALU.min,
+                    accum_out=negmax[:],
                 )
-            if len(sides(u)) == 2:
-                negmax = small.tile([P, 1], F32, name="negmax", tag="negmax")
-                nc.vector.tensor_tensor(out=negmax[:], in0=parts[:, PREV : PREV + 1], in1=parts[:, OWN : OWN + 1], op=ALU.min)
-                live[("negmax", u)] = negmax[:]
-            else:
-                live[("negmax", u)] = parts[:, OWN : OWN + 1]
+                running = negmax[:]
+            live[("neg_s", u)] = neg_s
+            live[("negmax", u)] = running
 
         def exponentials(u):
             n, h, i = units[u]
-            banks = live[("scores", u)]
             if i == 0:
-                sums = small.tile([P, QTILES, 2], F32, name="sums", tag="sums")
+                sums = small.tile([P, QTILES], F32, name="sums", tag="sums")
                 live[("sums", n, h)] = sums
             sums = live[("sums", n, h)]
-            for a in sides(u):
-                w = widths(u)[a]
-                nc.scalar.activation(
-                    out=e_tiles[i][:, a * CHUNK : a * CHUNK + w],
-                    in_=banks[a][:, :w],
-                    func=ACT.Exp,
-                    bias=live[("negmax", u)],
-                    scale=1.0,
-                    accum_out=sums[:, i, a : a + 1],
-                )
+            cols = slice(sides(u)[0] * CHUNK, CHUNK + (i + 1) * P)
+            nc.scalar.activation(
+                out=e_tiles[i][:, cols],
+                in_=live[("neg_s", u)][:, cols],
+                func=ACT.Exp,
+                bias=live[("negmax", u)],
+                scale=-1.0,
+                accum_out=sums[:, i : i + 1],
+            )
 
         def transposes(u):
             n, h, i = units[u]
@@ -293,12 +283,7 @@ def tile_localselfattention_pa_kernel(tc, q, k_scaled, hidden_states, Wv, out):
         def finish(n, h):
             sums = live[("sums", n, h)]
             recip = small.tile([P, QTILES], F32, name="recip", tag="recip")
-            if n == 0:
-                nc.vector.reciprocal(out=recip[:], in_=sums[:, :, OWN])
-            else:
-                den = small.tile([P, QTILES], F32, name="den", tag="den")
-                nc.vector.tensor_tensor(out=den[:], in0=sums[:, :, PREV], in1=sums[:, :, OWN], op=ALU.add)
-                nc.vector.reciprocal(out=recip[:], in_=den[:])
+            nc.vector.reciprocal(out=recip[:], in_=sums[:])
             o_sb = work.tile([P, QTILES, DH], F32, name="o_sb", tag="o_sb")
             nc.vector.tensor_tensor(
                 out=o_sb[:],
@@ -311,7 +296,6 @@ def tile_localselfattention_pa_kernel(tc, q, k_scaled, hidden_states, Wv, out):
                 in_=o_sb[:],
             )
 
-        ctx.enter_context(tc.manual_schedule())
         load_wv(0, 0)
         load_wv(1, 0)
         load_hidden(0)
@@ -324,56 +308,41 @@ def tile_localselfattention_pa_kernel(tc, q, k_scaled, hidden_states, Wv, out):
         load_qk(1, 1)
 
         for g in range(HID_PASSES):
-            wv_quantise(g, 0)
+            prep_wv(g, 0)
         for t in range(QTILES):
-            hidden_transposes(0, t, ps_et, "e_t")
-            hidden_copy(0, t)
-            hidden_quantise(0, t)
-        v_project(0, 0)
-        v_copy(0, 0)
-        v_quantise(0, 0)
-        qk_transposes(0, 0)
-        qk_copy(0, 0)
+            prep_hidden(0, t)
+        prep_v(0, 0)
+        prep_qk(0, 0)
 
         count = len(units)
         for step in range(count + 4):
-            front = step < count
-            if front:
+            if step < count:
                 n, h, i = units[step]
+                scores(step)
+                row_max(step)
                 nxt = step // QTILES + 1
-                more = nxt < len(groups)
-                hidden_next = h < QTILES and n + 1 < CHUNKS
                 if i == 0 and n == 1 and h == 0:
                     load_hidden(2)
                     load_qk(2, 0)
                     load_qk(2, 1)
-                scores(step)
-            if 0 <= step - 4 < count:
-                quantise(step - 4)
+                if i == 0 and nxt < len(groups):
+                    prep_qk(*groups[nxt])
+                if i == 1 and h < QTILES and n + 1 < CHUNKS:
+                    prep_hidden(n + 1, h)
+                if i == 2 and nxt < len(groups):
+                    prep_v(*groups[nxt])
+                if i == 3 and n == 0 and h < HID_PASSES:
+                    prep_wv(h, 1)
             if 0 <= step - 3 < count:
                 regroup(step - 3)
             if 0 <= step - 1 < count:
                 exponentials(step - 1)
-            if front and i == 0 and more:
-                qk_transposes(*groups[nxt])
-                qk_copy(*groups[nxt])
-            if front and i == 1 and hidden_next:
-                hidden_transposes(n + 1, h, ps_prep, "prep")
-                hidden_copy(n + 1, h)
             if 0 <= step - 2 < count:
                 transposes(step - 2)
-            if front and i == 2 and more:
-                v_project(*groups[nxt])
-                v_copy(*groups[nxt])
+            if 0 <= step - 3 < count:
+                quantise(step - 3)
             if 0 <= step - 4 < count:
                 multiply(step - 4)
-            if front and i == 2 and hidden_next:
-                hidden_quantise(n + 1, h)
-            if front and i == 3 and more:
-                v_quantise(*groups[nxt])
-            if front and i == 3 and n == 0 and h < HID_PASSES:
-                wv_quantise(h, 1)
-            if front:
-                row_max(step)
-            if 0 <= step - 4 < count and units[step - 4][2] == QTILES - 1:
-                finish(units[step - 4][0], units[step - 4][1])
+                n, h, i = units[step - 4]
+                if i == QTILES - 1:
+                    finish(n, h)

@@ -24,6 +24,8 @@ QTILES = CHUNK // P
 HID_PASSES = HID // K_PASS
 PREV, OWN = 0, 1
 MASKED = -1.0e9
+PAIRS = QTILES // 2
+FIRST_VALUES = 7
 
 FLOPS = 2 * SEQ * HID * WIDTH + 2 * 2 * HEADS * (2 * CHUNKS - 1) * CHUNK * CHUNK * DH
 
@@ -32,12 +34,13 @@ def tile_localselfattention_pa_kernel(tc, q, k_scaled, hidden_states, Wv, out):
     nc = tc.nc
     with ExitStack() as ctx:
         const = ctx.enter_context(tc.tile_pool(name="const", bufs=1))
-        raw = ctx.enter_context(tc.tile_pool(name="raw", bufs=2))
         keep = ctx.enter_context(tc.tile_pool(name="keep", bufs=1))
-        work = ctx.enter_context(tc.tile_pool(name="work", bufs=3))
-        small = ctx.enter_context(tc.tile_pool(name="small", bufs=6))
-        ahead = ctx.enter_context(tc.tile_pool(name="ahead", bufs=3))
-        ps_scores = ctx.enter_context(tc.psum_pool(name="ps_scores", bufs=2))
+        raw = ctx.enter_context(tc.tile_pool(name="raw", bufs=2))
+        work = ctx.enter_context(tc.tile_pool(name="work", bufs=2))
+        small = ctx.enter_context(tc.tile_pool(name="small", bufs=10))
+        ahead = ctx.enter_context(tc.tile_pool(name="ahead", bufs=4))
+        codes = ctx.enter_context(tc.tile_pool(name="codes", bufs=8))
+        ps_s = ctx.enter_context(tc.psum_pool(name="ps_s", bufs=4))
         ps_et = ctx.enter_context(tc.psum_pool(name="ps_et", bufs=2))
         ps_o = ctx.enter_context(tc.psum_pool(name="ps_o", bufs=1))
         ps_prep = ctx.enter_context(tc.psum_pool(name="ps_prep", bufs=1))
@@ -76,7 +79,7 @@ def tile_localselfattention_pa_kernel(tc, q, k_scaled, hidden_states, Wv, out):
         v_scales = keep.tile([P, CHUNKS, HEADS, DH], U8, name="v_scales", align_bytes=64)
         qk_t = keep.tile([P, CHUNKS, HEADS, 2, CHUNK], BF16, name="qk_t")
 
-        raw_tiles = {}
+        live = {}
 
         def load_wv(g, half):
             cols = slice(half * HALF, (half + 1) * HALF)
@@ -94,7 +97,7 @@ def tile_localselfattention_pa_kernel(tc, q, k_scaled, hidden_states, Wv, out):
                 out=hid_raw[:].rearrange("p (u ew) -> p u ew", u=2),
                 in_=hidden_states[0, rows, :].rearrange("(u p e) w -> p u (e w)", u=2, p=P, e=2),
             )
-            raw_tiles[("hid", n)] = hid_raw
+            live[("hid", n)] = hid_raw
 
         def load_qk(n, half):
             rows = slice(n * CHUNK, (n + 1) * CHUNK)
@@ -102,53 +105,69 @@ def tile_localselfattention_pa_kernel(tc, q, k_scaled, hidden_states, Wv, out):
             if half == 0:
                 q_raw = raw.tile([P, QTILES, WIDTH], BF16, name="q_raw", tag="q_raw")
                 k_raw = raw.tile([P, QTILES, WIDTH], BF16, name="k_raw", tag="k_raw")
-                raw_tiles[("q", n)] = q_raw
-                raw_tiles[("k", n)] = k_raw
-            nc.sync.dma_start(out=raw_tiles[("q", n)][:, :, cols], in_=q[0, rows, cols].rearrange("(r p) w -> p r w", p=P))
-            nc.sync.dma_start(out=raw_tiles[("k", n)][:, :, cols], in_=k_scaled[0, rows, cols].rearrange("(r p) w -> p r w", p=P))
+                live[("q", n)] = q_raw
+                live[("k", n)] = k_raw
+            nc.sync.dma_start(out=live[("q", n)][:, :, cols], in_=q[0, rows, cols].rearrange("(r p) w -> p r w", p=P))
+            nc.sync.dma_start(out=live[("k", n)][:, :, cols], in_=k_scaled[0, rows, cols].rearrange("(r p) w -> p r w", p=P))
 
-        def prep_wv(g, half):
+        def wv_group(g, half):
             cols = slice(half * HALF, (half + 1) * HALF)
             wv_grouped = work.tile([P, HALF, PACK], BF16, name="wv_grouped", tag="wv_grouped", align_bytes=64)
             nc.vector.tensor_copy(
                 out=wv_grouped[:].rearrange("p (c i) t -> p c t i", i=4),
                 in_=wv_raw[:, g, :, cols].rearrange("p t (c i) -> p c t i", i=4),
             )
+            live[("wv", g, half)] = wv_grouped
+
+        def wv_quantise(g, half):
+            cols = slice(half * HALF, (half + 1) * HALF)
             nc.vector.quantize_mx(
                 out=wv_codes[:, g, cols].bitcast(FP8X4),
                 scales=wv_scales[:, g, cols],
-                in_=wv_grouped[:].rearrange("p n t -> p (n t)"),
+                in_=live[("wv", g, half)][:].rearrange("p n t -> p (n t)"),
             )
 
-        def prep_hidden(n, t):
-            words = raw_tiles[("hid", n)][:].bitcast(F32)
-            hid_t = ps_prep.tile([P, PACK, P], F32, name="hid_t", tag="prep")
+        def hidden_turn(n, t):
+            words = live[("hid", n)][:].bitcast(F32)
+            hid_t = ps_s.tile([P, PACK, P], F32, name="hid_t", tag="s")
             for gu in range(PACK):
                 first = t * (HID // 2) + gu * P
                 nc.tensor.transpose(out=hid_t[:, gu, :], in_=words[:, first : first + P], identity=ident_f32[:])
+            live[("hid_t", n, t)] = hid_t
+
+        def hidden_group(n, t):
             hid_grouped = work.tile([P, HID_PASSES * P * PACK], BF16, name="hid_grouped", tag="hid_grouped", align_bytes=64)
             nc.scalar.copy(
                 out=hid_grouped[:].bitcast(F32).rearrange("p (g r u) -> p g r u", g=HID_PASSES, u=2),
-                in_=hid_t[:].rearrange("p (g u) r -> p g r u", g=HID_PASSES),
+                in_=live[("hid_t", n, t)][:].rearrange("p (g u) r -> p g r u", g=HID_PASSES),
             )
+            live[("hid_grouped", n, t)] = hid_grouped
+
+        def hidden_quantise(n, t):
             nc.vector.quantize_mx(
                 out=hid_codes[:, n, t, :].bitcast(FP8X4),
                 scales=hid_scales[:, n, t, :],
-                in_=hid_grouped[:],
+                in_=live[("hid_grouped", n, t)][:],
             )
 
-        def prep_qk(n, h):
+        def qk_turn(n, h):
             cols = slice(h * DH, (h + 1) * DH)
             qk_ps = ps_prep.tile([P, 2, CHUNK], BF16, name="qk_ps", tag="prep")
             for which, key in enumerate(("q", "k")):
-                src = raw_tiles[(key, n)]
+                src = live[(key, n)]
                 for r in range(QTILES):
                     nc.tensor.transpose(out=qk_ps[:, which, r * P : (r + 1) * P], in_=src[:, r, cols], identity=ident_bf[:])
-            nc.vector.tensor_copy(out=qk_t[:, n, h], in_=qk_ps[:])
+            live[("qk_ps", n, h)] = qk_ps
 
-        def prep_v(n, h):
+        def qk_keep(n, h):
+            nc.vector.tensor_copy(out=qk_t[:, n, h], in_=live[("qk_ps", n, h)][:])
+
+        def v_multiply(n, h):
             cols = slice(h * DH, (h + 1) * DH)
-            v_ps = ps_prep.tile([P, PACK, DH], F32, name="v_ps", tag="prep")
+            if n == 0:
+                v_ps = ps_s.tile([P, PACK, DH], F32, name="v_ps_s", tag="s")
+            else:
+                v_ps = ps_prep.tile([P, PACK, DH], F32, name="v_ps", tag="prep")
             for t in range(PACK):
                 for g in range(HID_PASSES):
                     nc.tensor.matmul_mx(
@@ -160,135 +179,144 @@ def tile_localselfattention_pa_kernel(tc, q, k_scaled, hidden_states, Wv, out):
                         start=(g == 0),
                         stop=(g == HID_PASSES - 1),
                     )
+            live[("v_ps", n, h)] = v_ps
+
+        def v_group(n, h):
             v_grouped = work.tile([P, DH, PACK], BF16, name="v_grouped", tag="v_grouped", align_bytes=64)
-            nc.scalar.copy(out=v_grouped[:], in_=v_ps[:].rearrange("p t d -> p d t"))
+            nc.scalar.copy(out=v_grouped[:], in_=live[("v_ps", n, h)][:].rearrange("p t d -> p d t"))
+            live[("v_grouped", n, h)] = v_grouped
+
+        def v_quantise(n, h):
             nc.vector.quantize_mx(
                 out=v_codes[:, n, h, :].bitcast(FP8X4),
                 scales=v_scales[:, n, h, :],
-                in_=v_grouped[:].rearrange("p d t -> p (d t)"),
+                in_=live[("v_grouped", n, h)][:].rearrange("p d t -> p (d t)"),
             )
 
         groups = [(n, h) for n in range(CHUNKS) for h in range(HEADS)]
-        units = [(n, h, i) for (n, h) in groups for i in range(QTILES)]
-        live = {}
+        pairs = [(n, h, i) for (n, h) in groups for i in range(0, QTILES, 2)]
 
-        def scores(u):
-            n, h, i = units[u]
-            q_cols = qk_t[:, n, h, 0, i * P : (i + 1) * P]
-            banks = {}
-            if n > 0:
-                s_prev = ps_scores.tile([P, CHUNK], F32, name="s_prev", tag="s_prev")
-                nc.tensor.matmul(out=s_prev[:], lhsT=q_cols, rhs=qk_t[:, n - 1, h, 1, :], start=True, stop=True)
-                banks[PREV] = s_prev
-            s_own = ps_scores.tile([P, CHUNK], F32, name="s_own", tag="s_own")
-            if i > 0:
-                nc.tensor.matmul(out=s_own[:, : i * P], lhsT=q_cols, rhs=qk_t[:, n, h, 1, : i * P], start=True, stop=True)
-            diag = slice(i * P, (i + 1) * P)
-            nc.tensor.matmul(out=s_own[:, diag], lhsT=ident_bf[:], rhs=mask_bf[:], start=True, stop=False)
-            nc.tensor.matmul(out=s_own[:, diag], lhsT=q_cols, rhs=qk_t[:, n, h, 1, diag], start=False, stop=True)
-            banks[OWN] = s_own
-            live[("scores", u)] = banks
+        def sides(n):
+            return (OWN,) if n == 0 else (PREV, OWN)
 
-        def widths(u):
-            n, h, i = units[u]
-            return {PREV: CHUNK, OWN: (i + 1) * P}
+        def scores(p):
+            n, h, i0 = pairs[p]
+            for a in sides(n):
+                for i in (i0, i0 + 1):
+                    q_cols = qk_t[:, n, h, 0, i * P : (i + 1) * P]
+                    s_ps = ps_s.tile([P, CHUNK], F32, name="s_ps", tag="s")
+                    live[("s", p, a, i)] = s_ps
+                    if a == PREV:
+                        nc.tensor.matmul(out=s_ps[:], lhsT=q_cols, rhs=qk_t[:, n - 1, h, 1, :], start=True, stop=True)
+                        continue
+                    if i > 0:
+                        nc.tensor.matmul(out=s_ps[:, : i * P], lhsT=q_cols, rhs=qk_t[:, n, h, 1, : i * P], start=True, stop=True)
+                    diag = slice(i * P, (i + 1) * P)
+                    nc.tensor.matmul(out=s_ps[:, diag], lhsT=q_cols, rhs=qk_t[:, n, h, 1, diag], start=True, stop=False)
+                    nc.tensor.matmul(out=s_ps[:, diag], lhsT=ident_bf[:], rhs=mask_bf[:], start=False, stop=True)
 
-        def sides(u):
-            return (OWN,) if units[u][0] == 0 else (PREV, OWN)
+        def row_max(p):
+            n, h, i0 = pairs[p]
+            running = {}
+            for a in sides(n):
+                for i in (i0, i0 + 1):
+                    w = CHUNK if a == PREV else (i + 1) * P
+                    if a == sides(n)[0]:
+                        neg_s = ahead.tile([P, 2 * CHUNK], F32, name="neg_s", tag="neg_s")
+                        live[("neg_s", p, i)] = neg_s
+                    negmax = small.tile([P, 1], F32, name="negmax%d" % a, tag="negmax%d" % a)
+                    nc.vector.tensor_scalar(
+                        out=live[("neg_s", p, i)][:, a * CHUNK : a * CHUNK + w],
+                        in0=live[("s", p, a, i)][:, :w],
+                        scalar1=-1.0,
+                        scalar2=running.get(i),
+                        op0=ALU.mult,
+                        op1=ALU.min,
+                        accum_out=negmax[:],
+                    )
+                    running[i] = negmax[:]
+                    live[("negmax", p, i)] = negmax
 
-        def row_max(u):
-            banks = live[("scores", u)]
-            neg_s = ahead.tile([P, 2 * CHUNK], F32, name="neg_s", tag="neg_s")
-            running = None
-            for a in sides(u):
-                w = widths(u)[a]
-                negmax = small.tile([P, 1], F32, name="negmax%d" % a, tag="negmax%d" % a)
-                nc.vector.tensor_scalar(
-                    out=neg_s[:, a * CHUNK : a * CHUNK + w],
-                    in0=banks[a][:, :w],
-                    scalar1=-1.0,
-                    scalar2=running,
-                    op0=ALU.mult,
-                    op1=ALU.min,
-                    accum_out=negmax[:],
-                )
-                running = negmax[:]
-            live[("neg_s", u)] = neg_s
-            live[("negmax", u)] = running
-
-        def exponentials(u):
-            n, h, i = units[u]
-            if i == 0:
+        def exponentials(p):
+            n, h, i0 = pairs[p]
+            if i0 == 0:
                 sums = small.tile([P, QTILES], F32, name="sums", tag="sums")
                 live[("sums", n, h)] = sums
-            sums = live[("sums", n, h)]
-            cols = slice(sides(u)[0] * CHUNK, CHUNK + (i + 1) * P)
-            nc.scalar.activation(
-                out=e_tiles[i][:, cols],
-                in_=live[("neg_s", u)][:, cols],
-                func=ACT.Exp,
-                bias=live[("negmax", u)],
-                scale=-1.0,
-                accum_out=sums[:, i : i + 1],
-            )
-
-        def transposes(u):
-            n, h, i = units[u]
-            e_t = ps_et.tile([P, 2, 2, P], F32, name="e_t", tag="e_t")
-            words = e_tiles[i][:].bitcast(F32)
-            for a in sides(u):
-                for half in range(2):
-                    first = (2 * a + half) * P
-                    nc.tensor.transpose(out=e_t[:, a, half, :], in_=words[:, first : first + P], identity=ident_f32[:])
-            live[("e_t", u)] = e_t
-
-        def regroup(u):
-            first = sides(u)[0]
-            e_grouped = work.tile([P, 2 * P * PACK], BF16, name="e_grouped", tag="e_grouped", align_bytes=64)
-            nc.scalar.copy(
-                out=e_grouped[:].bitcast(F32).rearrange("p (a r half) -> p a r half", a=2, half=2)[:, first:],
-                in_=live[("e_t", u)][:, first:].rearrange("p a half r -> p a r half"),
-            )
-            live[("e_grouped", u)] = e_grouped
-
-        def quantise(u):
-            first = sides(u)[0]
-            e_codes = work.tile([P, 2, P], U32, name="e_codes", tag="e_codes", align_bytes=64)
-            e_scales = work.tile([P, 2, P], U8, name="e_scales", tag="e_scales", align_bytes=64)
-            nc.vector.quantize_mx(
-                out=e_codes[:, first:].rearrange("p a r -> p (a r)").bitcast(FP8X4),
-                scales=e_scales[:, first:].rearrange("p a r -> p (a r)"),
-                in_=live[("e_grouped", u)][:, first * P * PACK :],
-            )
-            live[("e_codes", u)] = (e_codes, e_scales)
-
-        def multiply(u):
-            n, h, i = units[u]
-            if i == 0:
-                o_ps = ps_o.tile([P, QTILES, DH], F32, name="o_ps", tag="o_ps")
-                live[("o_ps", n, h)] = o_ps
-            o_ps = live[("o_ps", n, h)]
-            e_codes, e_scales = live[("e_codes", u)]
-            for a in sides(u):
-                nc.tensor.matmul_mx(
-                    out=o_ps[:, i, :],
-                    lhsT=e_codes[:, a, :].bitcast(FP8X4),
-                    lhsT_scale=e_scales[:, a, :],
-                    rhs=v_codes[:, n - 1 + a, h, :].bitcast(FP8X4),
-                    rhs_scale=v_scales[:, n - 1 + a, h, :],
-                    start=(a == sides(u)[0]),
-                    stop=(a == OWN),
+            for i in (i0, i0 + 1):
+                cols = slice(sides(n)[0] * CHUNK, CHUNK + (i + 1) * P)
+                nc.scalar.activation(
+                    out=e_tiles[i][:, cols],
+                    in_=live[("neg_s", p, i)][:, cols],
+                    func=ACT.Exp,
+                    bias=live[("negmax", p, i)][:],
+                    scale=-1.0,
+                    accum_out=live[("sums", n, h)][:, i : i + 1],
                 )
 
-        def finish(n, h):
-            sums = live[("sums", n, h)]
+        def turn(p):
+            n, h, i0 = pairs[p]
+            for i in (i0, i0 + 1):
+                words = e_tiles[i][:].bitcast(F32)
+                for a in sides(n):
+                    if n > 0 and a == PREV or n == 0 and i == i0:
+                        e_t = ps_et.tile([P, 2, 2, P], F32, name="e_t", tag="e_t")
+                    slot = i - i0 if n == 0 else a
+                    for half in range(2):
+                        first = (2 * a + half) * P
+                        nc.tensor.transpose(out=e_t[:, slot, half, :], in_=words[:, first : first + P], identity=ident_f32[:])
+                live[("e_t", p, i)] = e_t
+
+        def regroup(p):
+            n, h, i0 = pairs[p]
+            count = 1 if n == 0 else 2
+            e_grouped = work.tile([P, 4 * P * PACK], BF16, name="e_grouped", tag="e_grouped", align_bytes=64)
+            words = e_grouped[:].bitcast(F32).rearrange("p (b a r half) -> p b a r half", b=2, a=2, half=2)
+            for b in range(count):
+                nc.scalar.copy(out=words[:, b], in_=live[("e_t", p, i0 + b)][:].rearrange("p a half r -> p a r half"))
+            live[("e_grouped", p)] = e_grouped
+
+        def quantise(p):
+            n, h, i0 = pairs[p]
+            count = 1 if n == 0 else 2
+            e_codes = codes.tile([P, 2, 2, P], U32, name="e_codes", tag="e_codes", align_bytes=64)
+            e_scales = codes.tile([P, 2, 2, P], U8, name="e_scales", tag="e_scales", align_bytes=64)
+            nc.vector.quantize_mx(
+                out=e_codes[:, :count].rearrange("p b a r -> p (b a r)").bitcast(FP8X4),
+                scales=e_scales[:, :count].rearrange("p b a r -> p (b a r)"),
+                in_=live[("e_grouped", p)][:, : count * 2 * P * PACK],
+            )
+            live[("e_codes", p)] = (e_codes, e_scales)
+
+        def multiply(p):
+            n, h, i0 = pairs[p]
+            if i0 == 0:
+                o_ps = ps_o.tile([P, QTILES, DH], F32, name="o_ps", tag="o_ps")
+                live[("o_ps", n, h)] = o_ps
+            e_codes, e_scales = live[("e_codes", p)]
+            for i in (i0, i0 + 1):
+                for a in sides(n):
+                    b, slot = (0, i - i0) if n == 0 else (i - i0, a)
+                    nc.tensor.matmul_mx(
+                        out=live[("o_ps", n, h)][:, i, :],
+                        lhsT=e_codes[:, b, slot, :].bitcast(FP8X4),
+                        lhsT_scale=e_scales[:, b, slot, :],
+                        rhs=v_codes[:, n - 1 + a, h, :].bitcast(FP8X4),
+                        rhs_scale=v_scales[:, n - 1 + a, h, :],
+                        start=(a == sides(n)[0]),
+                        stop=(a == OWN),
+                    )
+
+        def invert(n, h):
             recip = small.tile([P, QTILES], F32, name="recip", tag="recip")
-            nc.vector.reciprocal(out=recip[:], in_=sums[:])
+            nc.vector.reciprocal(out=recip[:], in_=live[("sums", n, h)][:])
+            live[("recip", n, h)] = recip
+
+        def finish(n, h):
             o_sb = work.tile([P, QTILES, DH], F32, name="o_sb", tag="o_sb")
             nc.vector.tensor_tensor(
                 out=o_sb[:],
                 in0=live[("o_ps", n, h)][:],
-                in1=recip[:].unsqueeze(2).to_broadcast([P, QTILES, DH]),
+                in1=live[("recip", n, h)][:].unsqueeze(2).to_broadcast([P, QTILES, DH]),
                 op=ALU.mult,
             )
             nc.sync.dma_start(
@@ -296,53 +324,83 @@ def tile_localselfattention_pa_kernel(tc, q, k_scaled, hidden_states, Wv, out):
                 in_=o_sb[:],
             )
 
+        load_qk(0, 0)
         load_wv(0, 0)
         load_wv(1, 0)
         load_hidden(0)
-        load_qk(0, 0)
+        load_qk(0, 1)
         load_wv(0, 1)
         load_wv(1, 1)
-        load_qk(0, 1)
         load_hidden(1)
         load_qk(1, 0)
         load_qk(1, 1)
 
-        for g in range(HID_PASSES):
-            prep_wv(g, 0)
-        for t in range(QTILES):
-            prep_hidden(0, t)
-        prep_v(0, 0)
-        prep_qk(0, 0)
+        extra = {}
 
-        count = len(units)
-        for step in range(count + 4):
-            if step < count:
-                n, h, i = units[step]
-                scores(step)
-                row_max(step)
-                nxt = step // QTILES + 1
-                if i == 0 and n == 1 and h == 0:
+        def at(step, place, fn, *args):
+            extra.setdefault((step, place), []).append((fn, args))
+
+        def run(step, place):
+            for fn, args in extra.get((step, place), []):
+                fn(*args)
+
+        for g in range(HID_PASSES):
+            for half, first in ((0, 1), (1, FIRST_VALUES)):
+                at(first + g, "vector", wv_group, g, half)
+                at(first + g + 1, "vector", wv_quantise, g, half)
+        for n in range(CHUNKS):
+            for t in range(QTILES):
+                step = t + 1 if n == 0 else QTILES * n + t + 2
+                at(step, "turn", hidden_turn, n, t)
+                at(step + 1, "scalar", hidden_group, n, t)
+                at(step + 2, "vector", hidden_quantise, n, t)
+        v_step = []
+        for g, (n, h) in enumerate(groups):
+            step = max(PAIRS * g + 2, FIRST_VALUES + g)
+            v_step.append(step)
+            at(step, "multiply", v_multiply, n, h)
+            at(step, "scalar", v_group, n, h)
+            at(step + 1, "vector", v_quantise, n, h)
+            if g > 0:
+                at(PAIRS * (g - 1), "turn", qk_turn, n, h)
+                at(PAIRS * (g - 1) + 1, "vector", qk_keep, n, h)
+
+        count = len(pairs)
+        done = 0
+        with tc.manual_schedule():
+            qk_turn(0, 0)
+            qk_keep(0, 0)
+            for step in range(count + 5):
+                if step == 6:
                     load_hidden(2)
+                if step == PAIRS * HEADS:
                     load_qk(2, 0)
                     load_qk(2, 1)
-                if i == 0 and nxt < len(groups):
-                    prep_qk(*groups[nxt])
-                if i == 1 and h < QTILES and n + 1 < CHUNKS:
-                    prep_hidden(n + 1, h)
-                if i == 2 and nxt < len(groups):
-                    prep_v(*groups[nxt])
-                if i == 3 and n == 0 and h < HID_PASSES:
-                    prep_wv(h, 1)
-            if 0 <= step - 3 < count:
-                regroup(step - 3)
-            if 0 <= step - 1 < count:
-                exponentials(step - 1)
-            if 0 <= step - 2 < count:
-                transposes(step - 2)
-            if 0 <= step - 3 < count:
-                quantise(step - 3)
-            if 0 <= step - 4 < count:
-                multiply(step - 4)
-                n, h, i = units[step - 4]
-                if i == QTILES - 1:
-                    finish(n, h)
+                if 0 <= step - 1 < count:
+                    row_max(step - 1)
+                finished = None
+                while done <= step - 5 and v_step[done // PAIRS] + 2 <= step and finished is None:
+                    multiply(done)
+                    done += 1
+                    if done % PAIRS == 0:
+                        finished = groups[done // PAIRS - 1]
+                    if done == step - 4:
+                        break
+                run(step, "multiply")
+                if step < count:
+                    scores(step)
+                if 0 <= step - 2 < count:
+                    exponentials(step - 2)
+                if 0 <= step - 3 < count:
+                    regroup(step - 3)
+                run(step, "scalar")
+                if 0 <= step - 2 < count:
+                    turn(step - 2)
+                if finished:
+                    invert(*finished)
+                run(step, "vector")
+                run(step, "turn")
+                if finished:
+                    finish(*finished)
+                if 0 <= step - 3 < count:
+                    quantise(step - 3)

@@ -70,7 +70,6 @@ def tile_localselfattention_pa_kernel(tc, q, k_scaled, hidden_states, Wv, out):
                 nc.vector.memset(e_tile[:, OWN * CHUNK + (i + 1) * P :], 0.0)
             e_tiles.append(e_tile)
 
-        wv_raw = keep.tile([P, HID_PASSES, PACK, WIDTH], BF16, name="wv_raw")
         wv_codes = keep.tile([P, HID_PASSES, WIDTH], U32, name="wv_codes", align_bytes=64)
         wv_scales = keep.tile([P, HID_PASSES, WIDTH], U8, name="wv_scales", align_bytes=64)
         hid_codes = keep.tile([P, CHUNKS, QTILES, HID_PASSES * P], U32, name="hid_codes", align_bytes=64)
@@ -83,10 +82,12 @@ def tile_localselfattention_pa_kernel(tc, q, k_scaled, hidden_states, Wv, out):
 
         def load_wv(g, half):
             cols = slice(half * HALF, (half + 1) * HALF)
+            wv_raw = keep.tile([P, PACK, HALF], BF16, name="wv_raw%d%d" % (g, half))
+            live[("wv_raw", g, half)] = wv_raw
             for u in range(2):
                 first = g * K_PASS + u * 2 * P
                 nc.sync.dma_start(
-                    out=wv_raw[:, g, 2 * u : 2 * u + 2, cols],
+                    out=wv_raw[:, 2 * u : 2 * u + 2, :],
                     in_=Wv[first : first + 2 * P, cols].rearrange("(p e) n -> p e n", e=2),
                 )
 
@@ -111,11 +112,10 @@ def tile_localselfattention_pa_kernel(tc, q, k_scaled, hidden_states, Wv, out):
             nc.sync.dma_start(out=live[("k", n)][:, :, cols], in_=k_scaled[0, rows, cols].rearrange("(r p) w -> p r w", p=P))
 
         def wv_group(g, half):
-            cols = slice(half * HALF, (half + 1) * HALF)
             wv_grouped = work.tile([P, HALF, PACK], BF16, name="wv_grouped", tag="wv_grouped", align_bytes=64)
             nc.vector.tensor_copy(
                 out=wv_grouped[:].rearrange("p (c i) t -> p c t i", i=4),
-                in_=wv_raw[:, g, :, cols].rearrange("p t (c i) -> p c t i", i=4),
+                in_=live[("wv_raw", g, half)][:].rearrange("p t (c i) -> p c t i", i=4),
             )
             live[("wv", g, half)] = wv_grouped
 
@@ -161,6 +161,9 @@ def tile_localselfattention_pa_kernel(tc, q, k_scaled, hidden_states, Wv, out):
 
         def qk_keep(n, h):
             nc.vector.tensor_copy(out=qk_t[:, n, h], in_=live[("qk_ps", n, h)][:])
+
+        def qk_keep_scalar(n, h):
+            nc.scalar.copy(out=qk_t[:, n, h], in_=live[("qk_ps", n, h)][:])
 
         def v_multiply(n, h):
             cols = slice(h * DH, (h + 1) * DH)
@@ -363,7 +366,10 @@ def tile_localselfattention_pa_kernel(tc, q, k_scaled, hidden_states, Wv, out):
             at(step + 1, "vector", v_quantise, n, h)
             if g > 0:
                 at(PAIRS * (g - 1), "turn", qk_turn, n, h)
-                at(PAIRS * (g - 1) + 1, "vector", qk_keep, n, h)
+                if g % 2:
+                    at(PAIRS * (g - 1) + 1, "vector", qk_keep, n, h)
+                else:
+                    at(PAIRS * (g - 1) + 1, "scalar", qk_keep_scalar, n, h)
 
         count = len(pairs)
         done = 0

@@ -364,9 +364,10 @@ def tile_localselfattention_pa_kernel(tc, q, k_scaled, hidden_states, Wv, out):
             at(step, "multiply", v_multiply, n, h)
             at(step, "scalar", v_group, n, h)
             at(step + 1, "vector", v_quantise, n, h)
+            at(PAIRS * g + 4, "vector", invert, n, h)
             if g > 0:
                 at(PAIRS * (g - 1), "turn", qk_turn, n, h)
-                if g % 2:
+                if g % 3:
                     at(PAIRS * (g - 1) + 1, "vector", qk_keep, n, h)
                 else:
                     at(PAIRS * (g - 1) + 1, "scalar", qk_keep_scalar, n, h)
@@ -402,8 +403,6 @@ def tile_localselfattention_pa_kernel(tc, q, k_scaled, hidden_states, Wv, out):
                 run(step, "scalar")
                 if 0 <= step - 2 < count:
                     turn(step - 2)
-                if finished:
-                    invert(*finished)
                 run(step, "vector")
                 run(step, "turn")
                 if finished:

@@ -25,7 +25,7 @@ HID_PASSES = HID // K_PASS
 PREV, OWN = 0, 1
 MASKED = -1.0e9
 PAIRS = QTILES // 2
-FIRST_VALUES = 7
+FIRST_VALUES = 9
 
 FLOPS = 2 * SEQ * HID * WIDTH + 2 * 2 * HEADS * (2 * CHUNKS - 1) * CHUNK * CHUNK * DH
 
@@ -348,12 +348,12 @@ def tile_localselfattention_pa_kernel(tc, q, k_scaled, hidden_states, Wv, out):
                 fn(*args)
 
         for g in range(HID_PASSES):
-            for half, first in ((0, 1), (1, FIRST_VALUES)):
+            for half, first in ((0, 3), (1, FIRST_VALUES)):
                 at(first + g, "vector", wv_group, g, half)
                 at(first + g + 1, "vector", wv_quantise, g, half)
         for n in range(CHUNKS):
             for t in range(QTILES):
-                step = t + 1 if n == 0 else QTILES * n + t + 2
+                step = QTILES * n + t + 3
                 at(step, "turn", hidden_turn, n, t)
                 at(step + 1, "scalar", hidden_group, n, t)
                 at(step + 2, "vector", hidden_quantise, n, t)

@@ -39,7 +39,8 @@ def tile_localselfattention_pa_kernel(tc, q, k_scaled, hidden_states, Wv, out):
         work = ctx.enter_context(tc.tile_pool(name="work", bufs=2))
         small = ctx.enter_context(tc.tile_pool(name="small", bufs=10))
         ahead = ctx.enter_context(tc.tile_pool(name="ahead", bufs=4))
-        codes = ctx.enter_context(tc.tile_pool(name="codes", bufs=8))
+        grouped = ctx.enter_context(tc.tile_pool(name="grouped", bufs=3))
+        codes = ctx.enter_context(tc.tile_pool(name="codes", bufs=10))
         ps_s = ctx.enter_context(tc.psum_pool(name="ps_s", bufs=4))
         ps_et = ctx.enter_context(tc.psum_pool(name="ps_et", bufs=2))
         ps_o = ctx.enter_context(tc.psum_pool(name="ps_o", bufs=1))
@@ -49,19 +50,17 @@ def tile_localselfattention_pa_kernel(tc, q, k_scaled, hidden_states, Wv, out):
         make_identity(nc, ident_bf[:])
         ident_f32 = const.tile([P, P], F32, name="ident_f32")
         make_identity(nc, ident_f32[:])
-        mask_f32 = const.tile([P, P], F32, name="mask_f32")
-        nc.gpsimd.memset(mask_f32[:], 0.0)
+        mask_bf = const.tile([P, P], BF16, name="mask_bf")
+        nc.gpsimd.memset(mask_bf[:], 0.0)
         nc.gpsimd.affine_select(
-            out=mask_f32[:],
-            in_=mask_f32[:],
+            out=mask_bf[:],
+            in_=mask_bf[:],
             compare_op=ALU.is_ge,
             fill=MASKED,
             base=0,
             pattern=[[-1, P]],
             channel_multiplier=1,
         )
-        mask_bf = const.tile([P, P], BF16, name="mask_bf")
-        nc.vector.tensor_copy(out=mask_bf[:], in_=mask_f32[:])
 
         e_tiles = []
         for i in range(QTILES):
@@ -272,7 +271,7 @@ def tile_localselfattention_pa_kernel(tc, q, k_scaled, hidden_states, Wv, out):
         def regroup(p):
             n, h, i0 = pairs[p]
             count = 1 if n == 0 else 2
-            e_grouped = work.tile([P, 4 * P * PACK], BF16, name="e_grouped", tag="e_grouped", align_bytes=64)
+            e_grouped = grouped.tile([P, 4 * P * PACK], BF16, name="e_grouped", tag="e_grouped", align_bytes=64)
             words = e_grouped[:].bitcast(F32).rearrange("p (b a r half) -> p b a r half", b=2, a=2, half=2)
             for b in range(count):
                 nc.scalar.copy(out=words[:, b], in_=live[("e_t", p, i0 + b)][:].rearrange("p a half r -> p a r half"))
@@ -364,7 +363,7 @@ def tile_localselfattention_pa_kernel(tc, q, k_scaled, hidden_states, Wv, out):
             at(step, "multiply", v_multiply, n, h)
             at(step, "scalar", v_group, n, h)
             at(step + 1, "vector", v_quantise, n, h)
-            at(PAIRS * g + 4, "vector", invert, n, h)
+            at(PAIRS * g + 5, "vector", invert, n, h)
             if g > 0:
                 at(PAIRS * (g - 1), "turn", qk_turn, n, h)
                 if g % 3:
@@ -377,7 +376,7 @@ def tile_localselfattention_pa_kernel(tc, q, k_scaled, hidden_states, Wv, out):
         with tc.manual_schedule():
             qk_turn(0, 0)
             qk_keep(0, 0)
-            for step in range(count + 5):
+            for step in range(count + 6):
                 if step == 6:
                     load_hidden(2)
                 if step == PAIRS * HEADS:
@@ -386,12 +385,12 @@ def tile_localselfattention_pa_kernel(tc, q, k_scaled, hidden_states, Wv, out):
                 if 0 <= step - 1 < count:
                     row_max(step - 1)
                 finished = None
-                while done <= step - 5 and v_step[done // PAIRS] + 2 <= step and finished is None:
+                while done < count and done <= step - 6 and v_step[done // PAIRS] + 2 <= step and finished is None:
                     multiply(done)
                     done += 1
                     if done % PAIRS == 0:
                         finished = groups[done // PAIRS - 1]
-                    if done == step - 4:
+                    if done == step - 5:
                         break
                 run(step, "multiply")
                 if step < count:
@@ -407,5 +406,5 @@ def tile_localselfattention_pa_kernel(tc, q, k_scaled, hidden_states, Wv, out):
                 run(step, "turn")
                 if finished:
                     finish(*finished)
-                if 0 <= step - 3 < count:
-                    quantise(step - 3)
+                if 0 <= step - 4 < count:
+                    quantise(step - 4)

@@ -37,6 +37,7 @@ def tile_localselfattention_pa_kernel(tc, q, k_scaled, hidden_states, Wv, out):
         keep = ctx.enter_context(tc.tile_pool(name="keep", bufs=1))
         raw = ctx.enter_context(tc.tile_pool(name="raw", bufs=2))
         work = ctx.enter_context(tc.tile_pool(name="work", bufs=2))
+        store = ctx.enter_context(tc.tile_pool(name="store", bufs=3))
         small = ctx.enter_context(tc.tile_pool(name="small", bufs=10))
         ahead = ctx.enter_context(tc.tile_pool(name="ahead", bufs=4))
         grouped = ctx.enter_context(tc.tile_pool(name="grouped", bufs=3))
@@ -99,16 +100,17 @@ def tile_localselfattention_pa_kernel(tc, q, k_scaled, hidden_states, Wv, out):
             )
             live[("hid", n)] = hid_raw
 
-        def load_qk(n, half):
-            rows = slice(n * CHUNK, (n + 1) * CHUNK)
+        def load_qk(n, half, first=0, end=QTILES):
+            rows = slice(n * CHUNK + first * P, n * CHUNK + end * P)
             cols = slice(half * HALF, (half + 1) * HALF)
-            if half == 0:
+            tiles = slice(first, end)
+            if half == 0 and first == 0:
                 q_raw = raw.tile([P, QTILES, WIDTH], BF16, name="q_raw", tag="q_raw")
                 k_raw = raw.tile([P, QTILES, WIDTH], BF16, name="k_raw", tag="k_raw")
                 live[("q", n)] = q_raw
                 live[("k", n)] = k_raw
-            nc.sync.dma_start(out=live[("q", n)][:, :, cols], in_=q[0, rows, cols].rearrange("(r p) w -> p r w", p=P))
-            nc.sync.dma_start(out=live[("k", n)][:, :, cols], in_=k_scaled[0, rows, cols].rearrange("(r p) w -> p r w", p=P))
+            nc.sync.dma_start(out=live[("q", n)][:, tiles, cols], in_=q[0, rows, cols].rearrange("(r p) w -> p r w", p=P))
+            nc.sync.dma_start(out=live[("k", n)][:, tiles, cols], in_=k_scaled[0, rows, cols].rearrange("(r p) w -> p r w", p=P))
 
         def wv_group(g, half):
             wv_grouped = work.tile([P, HALF, PACK], BF16, name="wv_grouped", tag="wv_grouped", align_bytes=64)
@@ -149,20 +151,21 @@ def tile_localselfattention_pa_kernel(tc, q, k_scaled, hidden_states, Wv, out):
                 in_=live[("hid_grouped", n, t)][:],
             )
 
-        def qk_turn(n, h):
+        def qk_turn(n, h, first=0, end=QTILES):
             cols = slice(h * DH, (h + 1) * DH)
-            qk_ps = ps_prep.tile([P, 2, CHUNK], BF16, name="qk_ps", tag="prep")
+            if first > 0:
+                qk_ps = ps_s.tile([P, 2, CHUNK], BF16, name="qk_ps_s", tag="s")
+            else:
+                qk_ps = ps_prep.tile([P, 2, CHUNK], BF16, name="qk_ps", tag="prep")
             for which, key in enumerate(("q", "k")):
                 src = live[(key, n)]
-                for r in range(QTILES):
+                for r in range(first, end):
                     nc.tensor.transpose(out=qk_ps[:, which, r * P : (r + 1) * P], in_=src[:, r, cols], identity=ident_bf[:])
             live[("qk_ps", n, h)] = qk_ps
 
-        def qk_keep(n, h):
-            nc.vector.tensor_copy(out=qk_t[:, n, h], in_=live[("qk_ps", n, h)][:])
-
-        def qk_keep_scalar(n, h):
-            nc.scalar.copy(out=qk_t[:, n, h], in_=live[("qk_ps", n, h)][:])
+        def qk_keep(n, h, first=0, end=QTILES):
+            rows = slice(first * P, end * P)
+            nc.vector.tensor_copy(out=qk_t[:, n, h, :, rows], in_=live[("qk_ps", n, h)][:, :, rows])
 
         def v_multiply(n, h):
             cols = slice(h * DH, (h + 1) * DH)
@@ -197,6 +200,8 @@ def tile_localselfattention_pa_kernel(tc, q, k_scaled, hidden_states, Wv, out):
 
         groups = [(n, h) for n in range(CHUNKS) for h in range(HEADS)]
         pairs = [(n, h, i) for (n, h) in groups for i in range(0, QTILES, 2)]
+        pairs[-PAIRS:] = reversed(pairs[-PAIRS:])
+        last = len(pairs) - 1
 
         def sides(n):
             return (OWN,) if n == 0 else (PREV, OWN)
@@ -241,9 +246,10 @@ def tile_localselfattention_pa_kernel(tc, q, k_scaled, hidden_states, Wv, out):
 
         def exponentials(p):
             n, h, i0 = pairs[p]
-            if i0 == 0:
-                sums = small.tile([P, QTILES], F32, name="sums", tag="sums")
-                live[("sums", n, h)] = sums
+            g = p // PAIRS
+            if p % (2 * PAIRS) == 0:
+                sums = small.tile([P, 2 * QTILES], F32, name="sums", tag="sums")
+                live[("sums", g // 2)] = sums
             for i in (i0, i0 + 1):
                 cols = slice(sides(n)[0] * CHUNK, CHUNK + (i + 1) * P)
                 nc.scalar.activation(
@@ -252,7 +258,7 @@ def tile_localselfattention_pa_kernel(tc, q, k_scaled, hidden_states, Wv, out):
                     func=ACT.Exp,
                     bias=live[("negmax", p, i)][:],
                     scale=-1.0,
-                    accum_out=live[("sums", n, h)][:, i : i + 1],
+                    accum_out=live[("sums", g // 2)][:, g % 2 * QTILES + i : g % 2 * QTILES + i + 1],
                 )
 
         def turn(p):
@@ -274,7 +280,8 @@ def tile_localselfattention_pa_kernel(tc, q, k_scaled, hidden_states, Wv, out):
             e_grouped = grouped.tile([P, 4 * P * PACK], BF16, name="e_grouped", tag="e_grouped", align_bytes=64)
             words = e_grouped[:].bitcast(F32).rearrange("p (b a r half) -> p b a r half", b=2, a=2, half=2)
             for b in range(count):
-                nc.scalar.copy(out=words[:, b], in_=live[("e_t", p, i0 + b)][:].rearrange("p a half r -> p a r half"))
+                copy = nc.vector.tensor_copy if p == last - 2 or p == last - 1 and b == 0 else nc.scalar.copy
+                copy(out=words[:, b], in_=live[("e_t", p, i0 + b)][:].rearrange("p a half r -> p a r half"))
             live[("e_grouped", p)] = e_grouped
 
         def quantise(p):
@@ -282,16 +289,17 @@ def tile_localselfattention_pa_kernel(tc, q, k_scaled, hidden_states, Wv, out):
             count = 1 if n == 0 else 2
             e_codes = codes.tile([P, 2, 2, P], U32, name="e_codes", tag="e_codes", align_bytes=64)
             e_scales = codes.tile([P, 2, 2, P], U8, name="e_scales", tag="e_scales", align_bytes=64)
-            nc.vector.quantize_mx(
-                out=e_codes[:, :count].rearrange("p b a r -> p (b a r)").bitcast(FP8X4),
-                scales=e_scales[:, :count].rearrange("p b a r -> p (b a r)"),
-                in_=live[("e_grouped", p)][:, : count * 2 * P * PACK],
-            )
+            for first, end in [(0, 1), (1, 2)] if p == last else [(0, count)]:
+                nc.vector.quantize_mx(
+                    out=e_codes[:, first:end].rearrange("p b a r -> p (b a r)").bitcast(FP8X4),
+                    scales=e_scales[:, first:end].rearrange("p b a r -> p (b a r)"),
+                    in_=live[("e_grouped", p)][:, first * 2 * P * PACK : end * 2 * P * PACK],
+                )
             live[("e_codes", p)] = (e_codes, e_scales)
 
         def multiply(p):
             n, h, i0 = pairs[p]
-            if i0 == 0:
+            if p % PAIRS == 0:
                 o_ps = ps_o.tile([P, QTILES, DH], F32, name="o_ps", tag="o_ps")
                 live[("o_ps", n, h)] = o_ps
             e_codes, e_scales = live[("e_codes", p)]
@@ -308,25 +316,40 @@ def tile_localselfattention_pa_kernel(tc, q, k_scaled, hidden_states, Wv, out):
                         stop=(a == OWN),
                     )
 
-        def invert(n, h):
-            recip = small.tile([P, QTILES], F32, name="recip", tag="recip")
-            nc.vector.reciprocal(out=recip[:], in_=live[("sums", n, h)][:])
-            live[("recip", n, h)] = recip
+        def invert(g):
+            recip = small.tile([P, 2 * QTILES], F32, name="recip", tag="recip")
+            nc.vector.reciprocal(out=recip[:], in_=live[("sums", g // 2)][:])
+            for k in range(2):
+                live[("recip",) + groups[g - 1 + k]] = recip[:, k * QTILES : (k + 1) * QTILES]
 
-        def finish(n, h):
-            o_sb = work.tile([P, QTILES, DH], F32, name="o_sb", tag="o_sb")
+        def put(n, h, first, end, o_sb):
+            rows = slice(n * CHUNK + first * P, n * CHUNK + end * P)
+            nc.sync.dma_start(
+                out=out[0, rows, h * DH : (h + 1) * DH].rearrange("(i p) d -> p i d", p=P),
+                in_=o_sb[:, first:end],
+            )
+
+        def finish(n, h, first=0, end=QTILES):
+            o_sb = store.tile([P, QTILES, DH], F32, name="o_sb", tag="o_sb")
+            tiles = slice(first, end)
             nc.vector.tensor_tensor(
-                out=o_sb[:],
-                in0=live[("o_ps", n, h)][:],
-                in1=live[("recip", n, h)][:].unsqueeze(2).to_broadcast([P, QTILES, DH]),
+                out=o_sb[:, tiles],
+                in0=live[("o_ps", n, h)][:, tiles],
+                in1=live[("recip", n, h)][:, tiles].unsqueeze(2).to_broadcast([P, end - first, DH]),
                 op=ALU.mult,
             )
-            nc.sync.dma_start(
-                out=out[0, n * CHUNK : (n + 1) * CHUNK, h * DH : (h + 1) * DH].rearrange("(i p) d -> p i d", p=P),
-                in_=o_sb[:],
-            )
+            put(n, h, first, end, o_sb)
 
-        load_qk(0, 0)
+        def finish_scalar(n, h, first=0, end=QTILES):
+            o_sb = store.tile([P, QTILES, DH], F32, name="o_sb", tag="o_sb")
+            for i in range(first, end):
+                nc.scalar.activation(
+                    out=o_sb[:, i, :], in_=live[("o_ps", n, h)][:, i, :], func=ACT.Copy, scale=live[("recip", n, h)][:, i : i + 1]
+                )
+            put(n, h, first, end, o_sb)
+
+        load_qk(0, 0, 0, 2)
+        load_qk(0, 0, 2, QTILES)
         load_wv(0, 0)
         load_wv(1, 0)
         load_hidden(0)
@@ -359,24 +382,24 @@ def tile_localselfattention_pa_kernel(tc, q, k_scaled, hidden_states, Wv, out):
         v_step = []
         for g, (n, h) in enumerate(groups):
             step = max(PAIRS * g + 2, FIRST_VALUES + g)
+            if g == len(groups) - 1:
+                step -= 1
             v_step.append(step)
             at(step, "multiply", v_multiply, n, h)
             at(step, "scalar", v_group, n, h)
             at(step + 1, "vector", v_quantise, n, h)
-            at(PAIRS * g + 5, "vector", invert, n, h)
+            if g % 2:
+                at(PAIRS * g + 4, "vector", invert, g)
             if g > 0:
                 at(PAIRS * (g - 1), "turn", qk_turn, n, h)
-                if g % 3:
-                    at(PAIRS * (g - 1) + 1, "vector", qk_keep, n, h)
-                else:
-                    at(PAIRS * (g - 1) + 1, "scalar", qk_keep_scalar, n, h)
+                at(PAIRS * (g - 1) + 1, "vector", qk_keep, n, h)
 
         count = len(pairs)
         done = 0
         with tc.manual_schedule():
-            qk_turn(0, 0)
-            qk_keep(0, 0)
-            for step in range(count + 6):
+            qk_turn(0, 0, 0, 2)
+            qk_keep(0, 0, 0, 2)
+            for step in range(count):
                 if step == 6:
                     load_hidden(2)
                 if step == PAIRS * HEADS:
@@ -384,8 +407,10 @@ def tile_localselfattention_pa_kernel(tc, q, k_scaled, hidden_states, Wv, out):
                     load_qk(2, 1)
                 if 0 <= step - 1 < count:
                     row_max(step - 1)
+                if step == 1:
+                    qk_keep(0, 0, 2, QTILES)
                 finished = None
-                while done < count and done <= step - 6 and v_step[done // PAIRS] + 2 <= step and finished is None:
+                while done <= step - 6 and v_step[done // PAIRS] + 2 <= step and finished is None:
                     multiply(done)
                     done += 1
                     if done % PAIRS == 0:
@@ -395,6 +420,8 @@ def tile_localselfattention_pa_kernel(tc, q, k_scaled, hidden_states, Wv, out):
                 run(step, "multiply")
                 if step < count:
                     scores(step)
+                if step == 0:
+                    qk_turn(0, 0, 2, QTILES)
                 if 0 <= step - 2 < count:
                     exponentials(step - 2)
                 if 0 <= step - 3 < count:
@@ -408,3 +435,28 @@ def tile_localselfattention_pa_kernel(tc, q, k_scaled, hidden_states, Wv, out):
                     finish(*finished)
                 if 0 <= step - 4 < count:
                     quantise(step - 4)
+
+            row_max(last)
+            multiply(last - 5)
+            multiply(last - 4)
+            exponentials(last - 1)
+            regroup(last - 2)
+            turn(last - 1)
+            exponentials(last)
+            v_quantise(*groups[-1])
+            regroup(last - 1)
+            quantise(last - 3)
+            turn(last)
+            finish(*groups[-3])
+            quantise(last - 2)
+            multiply(last - 3)
+            multiply(last - 2)
+            regroup(last)
+            invert(len(groups) - 1)
+            quantise(last - 1)
+            finish_scalar(*groups[-2])
+            quantise(last)
+            multiply(last - 1)
+            multiply(last)
+            finish_scalar(*groups[-1], 2, QTILES)
+            finish(*groups[-1], 0, 2)

@@ -39,9 +39,9 @@ def tile_localselfattention_pa_kernel(tc, q, k_scaled, hidden_states, Wv, out):
         work = ctx.enter_context(tc.tile_pool(name="work", bufs=2))
         store = ctx.enter_context(tc.tile_pool(name="store", bufs=3))
         small = ctx.enter_context(tc.tile_pool(name="small", bufs=10))
-        ahead = ctx.enter_context(tc.tile_pool(name="ahead", bufs=4))
+        ahead = ctx.enter_context(tc.tile_pool(name="ahead", bufs=6))
         grouped = ctx.enter_context(tc.tile_pool(name="grouped", bufs=3))
-        codes = ctx.enter_context(tc.tile_pool(name="codes", bufs=10))
+        codes = ctx.enter_context(tc.tile_pool(name="codes", bufs=8))
         ps_s = ctx.enter_context(tc.psum_pool(name="ps_s", bufs=4))
         ps_et = ctx.enter_context(tc.psum_pool(name="ps_et", bufs=2))
         ps_o = ctx.enter_context(tc.psum_pool(name="ps_o", bufs=1))
@@ -167,6 +167,9 @@ def tile_localselfattention_pa_kernel(tc, q, k_scaled, hidden_states, Wv, out):
             rows = slice(first * P, end * P)
             nc.vector.tensor_copy(out=qk_t[:, n, h, :, rows], in_=live[("qk_ps", n, h)][:, :, rows])
 
+        def qk_keep_scalar(n, h):
+            nc.scalar.copy(out=qk_t[:, n, h], in_=live[("qk_ps", n, h)][:])
+
         def v_multiply(n, h):
             cols = slice(h * DH, (h + 1) * DH)
             if n == 0:
@@ -224,7 +227,7 @@ def tile_localselfattention_pa_kernel(tc, q, k_scaled, hidden_states, Wv, out):
 
         def row_max(p):
             n, h, i0 = pairs[p]
-            running = {}
+            minima = {}
             for a in sides(n):
                 for i in (i0, i0 + 1):
                     w = CHUNK if a == PREV else (i + 1) * P
@@ -236,13 +239,21 @@ def tile_localselfattention_pa_kernel(tc, q, k_scaled, hidden_states, Wv, out):
                         out=live[("neg_s", p, i)][:, a * CHUNK : a * CHUNK + w],
                         in0=live[("s", p, a, i)][:, :w],
                         scalar1=-1.0,
-                        scalar2=running.get(i),
+                        scalar2=None,
                         op0=ALU.mult,
                         op1=ALU.min,
                         accum_out=negmax[:],
                     )
-                    running[i] = negmax[:]
-                    live[("negmax", p, i)] = negmax
+                    minima[a, i] = negmax
+            for i in (i0, i0 + 1):
+                if n == 0:
+                    live[("negmax", p, i)] = minima[OWN, i]
+                    continue
+                both = small.tile([P, 1], F32, name="both", tag="both")
+                nc.gpsimd.tensor_scalar(
+                    out=both[:], in0=minima[PREV, i][:], scalar1=minima[OWN, i][:], scalar2=None, op0=ALU.min
+                )
+                live[("negmax", p, i)] = both
 
         def exponentials(p):
             n, h, i0 = pairs[p]
@@ -392,7 +403,10 @@ def tile_localselfattention_pa_kernel(tc, q, k_scaled, hidden_states, Wv, out):
                 at(PAIRS * g + 4, "vector", invert, g)
             if g > 0:
                 at(PAIRS * (g - 1), "turn", qk_turn, n, h)
-                at(PAIRS * (g - 1) + 1, "vector", qk_keep, n, h)
+                if g % 2:
+                    at(PAIRS * (g - 1) + 1, "vector", qk_keep, n, h)
+                else:
+                    at(PAIRS * (g - 1) + 1, "scalar", qk_keep_scalar, n, h)
 
         count = len(pairs)
         done = 0

from contextlib import ExitStack

import concourse.mybir as mybir
from concourse.masks import make_identity

BF16 = mybir.dt.bfloat16
F32 = mybir.dt.float32
U32 = mybir.dt.uint32
U8 = mybir.dt.uint8
FP8X4 = mybir.dt.float8_e4m3fn_x4
ALU = mybir.AluOpType
ACT = mybir.ActivationFunctionType
AX = mybir.AxisListType

P = 128
PACK = 4
K_PASS = P * PACK

SEQ, HID, HEADS, DH, CHUNK = 1536, 1024, 8, 128, 512
WIDTH = HEADS * DH
HALF = WIDTH // 2
CHUNKS = SEQ // CHUNK
QTILES = CHUNK // P
HID_PASSES = HID // K_PASS
PREV, OWN = 0, 1
MASKED = -1.0e9
PAIRS = QTILES // 2
FIRST_VALUES = 9

FLOPS = 2 * SEQ * HID * WIDTH + 2 * 2 * HEADS * (2 * CHUNKS - 1) * CHUNK * CHUNK * DH


def tile_localselfattention_pa_kernel(tc, q, k_scaled, hidden_states, Wv, out):
    nc = tc.nc
    with ExitStack() as ctx:
        const = ctx.enter_context(tc.tile_pool(name="const", bufs=1))
        keep = ctx.enter_context(tc.tile_pool(name="keep", bufs=1))
        raw = ctx.enter_context(tc.tile_pool(name="raw", bufs=2))
        work = ctx.enter_context(tc.tile_pool(name="work", bufs=2))
        store = ctx.enter_context(tc.tile_pool(name="store", bufs=3))
        small = ctx.enter_context(tc.tile_pool(name="small", bufs=10))
        ahead = ctx.enter_context(tc.tile_pool(name="ahead", bufs=6))
        grouped = ctx.enter_context(tc.tile_pool(name="grouped", bufs=3))
        codes = ctx.enter_context(tc.tile_pool(name="codes", bufs=8))
        ps_s = ctx.enter_context(tc.psum_pool(name="ps_s", bufs=4))
        ps_et = ctx.enter_context(tc.psum_pool(name="ps_et", bufs=2))
        ps_o = ctx.enter_context(tc.psum_pool(name="ps_o", bufs=1))
        ps_prep = ctx.enter_context(tc.psum_pool(name="ps_prep", bufs=1))

        ident_bf = const.tile([P, P], BF16, name="ident_bf")
        make_identity(nc, ident_bf[:])
        ident_f32 = const.tile([P, P], F32, name="ident_f32")
        make_identity(nc, ident_f32[:])
        mask_bf = const.tile([P, P], BF16, name="mask_bf")
        nc.gpsimd.memset(mask_bf[:], 0.0)
        nc.gpsimd.affine_select(
            out=mask_bf[:],
            in_=mask_bf[:],
            compare_op=ALU.is_ge,
            fill=MASKED,
            base=0,
            pattern=[[-1, P]],
            channel_multiplier=1,
        )

        e_tiles = []
        for i in range(QTILES):
            e_tile = keep.tile([P, 2 * CHUNK], BF16, name="e_tile%d" % i)
            if (i + 1) * P < CHUNK:
                nc.vector.memset(e_tile[:, OWN * CHUNK + (i + 1) * P :], 0.0)
            e_tiles.append(e_tile)

        wv_codes = keep.tile([P, HID_PASSES, WIDTH], U32, name="wv_codes", align_bytes=64)
        wv_scales = keep.tile([P, HID_PASSES, WIDTH], U8, name="wv_scales", align_bytes=64)
        hid_codes = keep.tile([P, CHUNKS, QTILES, HID_PASSES * P], U32, name="hid_codes", align_bytes=64)
        hid_scales = keep.tile([P, CHUNKS, QTILES, HID_PASSES * P], U8, name="hid_scales", align_bytes=64)
        v_codes = keep.tile([P, CHUNKS, HEADS, DH], U32, name="v_codes", align_bytes=64)
        v_scales = keep.tile([P, CHUNKS, HEADS, DH], U8, name="v_scales", align_bytes=64)
        qk_t = keep.tile([P, CHUNKS, HEADS, 2, CHUNK], BF16, name="qk_t")

        live = {}

        def load_wv(g, half):
            cols = slice(half * HALF, (half + 1) * HALF)
            wv_raw = keep.tile([P, PACK, HALF], BF16, name="wv_raw%d%d" % (g, half))
            live[("wv_raw", g, half)] = wv_raw
            for u in range(2):
                first = g * K_PASS + u * 2 * P
                nc.sync.dma_start(
                    out=wv_raw[:, 2 * u : 2 * u + 2, :],
                    in_=Wv[first : first + 2 * P, cols].rearrange("(p e) n -> p e n", e=2),
                )

        def load_hidden(n):
            rows = slice(n * CHUNK, (n + 1) * CHUNK)
            hid_raw = raw.tile([P, QTILES * HID], BF16, name="hid_raw", tag="hid_raw")
            nc.sync.dma_start(
                out=hid_raw[:].rearrange("p (u ew) -> p u ew", u=2),
                in_=hidden_states[0, rows, :].rearrange("(u p e) w -> p u (e w)", u=2, p=P, e=2),
            )
            live[("hid", n)] = hid_raw

        def load_qk(n, half, first=0, end=QTILES):
            rows = slice(n * CHUNK + first * P, n * CHUNK + end * P)
            cols = slice(half * HALF, (half + 1) * HALF)
            tiles = slice(first, end)
            if half == 0 and first == 0:
                q_raw = raw.tile([P, QTILES, WIDTH], BF16, name="q_raw", tag="q_raw")
                k_raw = raw.tile([P, QTILES, WIDTH], BF16, name="k_raw", tag="k_raw")
                live[("q", n)] = q_raw
                live[("k", n)] = k_raw
            nc.sync.dma_start(out=live[("q", n)][:, tiles, cols], in_=q[0, rows, cols].rearrange("(r p) w -> p r w", p=P))
            nc.sync.dma_start(out=live[("k", n)][:, tiles, cols], in_=k_scaled[0, rows, cols].rearrange("(r p) w -> p r w", p=P))

        def wv_group(g, half):
            wv_grouped = work.tile([P, HALF, PACK], BF16, name="wv_grouped", tag="wv_grouped", align_bytes=64)
            nc.vector.tensor_copy(
                out=wv_grouped[:].rearrange("p (c i) t -> p c t i", i=4),
                in_=live[("wv_raw", g, half)][:].rearrange("p t (c i) -> p c t i", i=4),
            )
            live[("wv", g, half)] = wv_grouped

        def wv_quantise(g, half):
            cols = slice(half * HALF, (half + 1) * HALF)
            nc.vector.quantize_mx(
                out=wv_codes[:, g, cols].bitcast(FP8X4),
                scales=wv_scales[:, g, cols],
                in_=live[("wv", g, half)][:].rearrange("p n t -> p (n t)"),
            )

        def hidden_turn(n, t):
            words = live[("hid", n)][:].bitcast(F32)
            hid_t = ps_s.tile([P, PACK, P], F32, name="hid_t", tag="s")
            for gu in range(PACK):
                first = t * (HID // 2) + gu * P
                nc.tensor.transpose(out=hid_t[:, gu, :], in_=words[:, first : first + P], identity=ident_f32[:])
            live[("hid_t", n, t)] = hid_t

        def hidden_group(n, t):
            hid_grouped = work.tile([P, HID_PASSES * P * PACK], BF16, name="hid_grouped", tag="hid_grouped", align_bytes=64)
            nc.scalar.copy(
                out=hid_grouped[:].bitcast(F32).rearrange("p (g r u) -> p g r u", g=HID_PASSES, u=2),
                in_=live[("hid_t", n, t)][:].rearrange("p (g u) r -> p g r u", g=HID_PASSES),
            )
            live[("hid_grouped", n, t)] = hid_grouped

        def hidden_quantise(n, t):
            nc.vector.quantize_mx(
                out=hid_codes[:, n, t, :].bitcast(FP8X4),
                scales=hid_scales[:, n, t, :],
                in_=live[("hid_grouped", n, t)][:],
            )

        def qk_turn(n, h, first=0, end=QTILES):
            cols = slice(h * DH, (h + 1) * DH)
            if first > 0:
                qk_ps = ps_s.tile([P, 2, CHUNK], BF16, name="qk_ps_s", tag="s")
            else:
                qk_ps = ps_prep.tile([P, 2, CHUNK], BF16, name="qk_ps", tag="prep")
            for which, key in enumerate(("q", "k")):
                src = live[(key, n)]
                for r in range(first, end):
                    nc.tensor.transpose(out=qk_ps[:, which, r * P : (r + 1) * P], in_=src[:, r, cols], identity=ident_bf[:])
            live[("qk_ps", n, h)] = qk_ps

        def qk_keep(n, h, first=0, end=QTILES):
            rows = slice(first * P, end * P)
            nc.vector.tensor_copy(out=qk_t[:, n, h, :, rows], in_=live[("qk_ps", n, h)][:, :, rows])

        def qk_keep_scalar(n, h):
            nc.scalar.copy(out=qk_t[:, n, h], in_=live[("qk_ps", n, h)][:])

        def v_multiply(n, h):
            cols = slice(h * DH, (h + 1) * DH)
            if n == 0:
                v_ps = ps_s.tile([P, PACK, DH], F32, name="v_ps_s", tag="s")
            else:
                v_ps = ps_prep.tile([P, PACK, DH], F32, name="v_ps", tag="prep")
            for t in range(PACK):
                for g in range(HID_PASSES):
                    nc.tensor.matmul_mx(
                        out=v_ps[:, t, :],
                        lhsT=hid_codes[:, n, t, g * P : (g + 1) * P].bitcast(FP8X4),
                        lhsT_scale=hid_scales[:, n, t, g * P : (g + 1) * P],
                        rhs=wv_codes[:, g, cols].bitcast(FP8X4),
                        rhs_scale=wv_scales[:, g, cols],
                        start=(g == 0),
                        stop=(g == HID_PASSES - 1),
                    )
            live[("v_ps", n, h)] = v_ps

        def v_group(n, h):
            v_grouped = work.tile([P, DH, PACK], BF16, name="v_grouped", tag="v_grouped", align_bytes=64)
            nc.scalar.copy(out=v_grouped[:], in_=live[("v_ps", n, h)][:].rearrange("p t d -> p d t"))
            live[("v_grouped", n, h)] = v_grouped

        def v_quantise(n, h):
            nc.vector.quantize_mx(
                out=v_codes[:, n, h, :].bitcast(FP8X4),
                scales=v_scales[:, n, h, :],
                in_=live[("v_grouped", n, h)][:].rearrange("p d t -> p (d t)"),
            )

        groups = [(n, h) for n in range(CHUNKS) for h in range(HEADS)]
        pairs = [(n, h, i) for (n, h) in groups for i in range(0, QTILES, 2)]
        pairs[-PAIRS:] = reversed(pairs[-PAIRS:])
        last = len(pairs) - 1

        def sides(n):
            return (OWN,) if n == 0 else (PREV, OWN)

        def scores(p):
            n, h, i0 = pairs[p]
            for a in sides(n):
                for i in (i0, i0 + 1):
                    q_cols = qk_t[:, n, h, 0, i * P : (i + 1) * P]
                    s_ps = ps_s.tile([P, CHUNK], F32, name="s_ps", tag="s")
                    live[("s", p, a, i)] = s_ps
                    if a == PREV:
                        nc.tensor.matmul(out=s_ps[:], lhsT=q_cols, rhs=qk_t[:, n - 1, h, 1, :], start=True, stop=True)
                        continue
                    if i > 0:
                        nc.tensor.matmul(out=s_ps[:, : i * P], lhsT=q_cols, rhs=qk_t[:, n, h, 1, : i * P], start=True, stop=True)
                    diag = slice(i * P, (i + 1) * P)
                    nc.tensor.matmul(out=s_ps[:, diag], lhsT=q_cols, rhs=qk_t[:, n, h, 1, diag], start=True, stop=False)
                    nc.tensor.matmul(out=s_ps[:, diag], lhsT=ident_bf[:], rhs=mask_bf[:], start=False, stop=True)

        def row_max(p):
            n, h, i0 = pairs[p]
            minima = {}
            for a in sides(n):
                for i in (i0, i0 + 1):
                    w = CHUNK if a == PREV else (i + 1) * P
                    if a == sides(n)[0]:
                        neg_s = ahead.tile([P, 2 * CHUNK], F32, name="neg_s", tag="neg_s")
                        live[("neg_s", p, i)] = neg_s
                    negmax = small.tile([P, 1], F32, name="negmax%d" % a, tag="negmax%d" % a)
                    nc.vector.tensor_scalar(
                        out=live[("neg_s", p, i)][:, a * CHUNK : a * CHUNK + w],
                        in0=live[("s", p, a, i)][:, :w],
                        scalar1=-1.0,
                        scalar2=None,
                        op0=ALU.mult,
                        op1=ALU.min,
                        accum_out=negmax[:],
                    )
                    minima[a, i] = negmax
            for i in (i0, i0 + 1):
                if n == 0:
                    live[("negmax", p, i)] = minima[OWN, i]
                    continue
                both = small.tile([P, 1], F32, name="both", tag="both")
                nc.gpsimd.tensor_scalar(
                    out=both[:], in0=minima[PREV, i][:], scalar1=minima[OWN, i][:], scalar2=None, op0=ALU.min
                )
                live[("negmax", p, i)] = both

        def exponentials(p):
            n, h, i0 = pairs[p]
            g = p // PAIRS
            if p % (2 * PAIRS) == 0:
                sums = small.tile([P, 2 * QTILES], F32, name="sums", tag="sums")
                live[("sums", g // 2)] = sums
            for i in (i0, i0 + 1):
                cols = slice(sides(n)[0] * CHUNK, CHUNK + (i + 1) * P)
                nc.scalar.activation(
                    out=e_tiles[i][:, cols],
                    in_=live[("neg_s", p, i)][:, cols],
                    func=ACT.Exp,
                    bias=live[("negmax", p, i)][:],
                    scale=-1.0,
                    accum_out=live[("sums", g // 2)][:, g % 2 * QTILES + i : g % 2 * QTILES + i + 1],
                )

        def turn(p):
            n, h, i0 = pairs[p]
            for i in (i0, i0 + 1):
                words = e_tiles[i][:].bitcast(F32)
                for a in sides(n):
                    if n > 0 and a == PREV or n == 0 and i == i0:
                        e_t = ps_et.tile([P, 2, 2, P], F32, name="e_t", tag="e_t")
                    slot = i - i0 if n == 0 else a
                    for half in range(2):
                        first = (2 * a + half) * P
                        nc.tensor.transpose(out=e_t[:, slot, half, :], in_=words[:, first : first + P], identity=ident_f32[:])
                live[("e_t", p, i)] = e_t

        def regroup(p):
            n, h, i0 = pairs[p]
            count = 1 if n == 0 else 2
            e_grouped = grouped.tile([P, 4 * P * PACK], BF16, name="e_grouped", tag="e_grouped", align_bytes=64)
            words = e_grouped[:].bitcast(F32).rearrange("p (b a r half) -> p b a r half", b=2, a=2, half=2)
            for b in range(count):
                copy = nc.vector.tensor_copy if p == last - 2 or p == last - 1 and b == 0 else nc.scalar.copy
                copy(out=words[:, b], in_=live[("e_t", p, i0 + b)][:].rearrange("p a half r -> p a r half"))
            live[("e_grouped", p)] = e_grouped

        def quantise(p):
            n, h, i0 = pairs[p]
            count = 1 if n == 0 else 2
            e_codes = codes.tile([P, 2, 2, P], U32, name="e_codes", tag="e_codes", align_bytes=64)
            e_scales = codes.tile([P, 2, 2, P], U8, name="e_scales", tag="e_scales", align_bytes=64)
            for first, end in [(0, 1), (1, 2)] if p == last else [(0, count)]:
                nc.vector.quantize_mx(
                    out=e_codes[:, first:end].rearrange("p b a r -> p (b a r)").bitcast(FP8X4),
                    scales=e_scales[:, first:end].rearrange("p b a r -> p (b a r)"),
                    in_=live[("e_grouped", p)][:, first * 2 * P * PACK : end * 2 * P * PACK],
                )
            live[("e_codes", p)] = (e_codes, e_scales)

        def multiply(p):
            n, h, i0 = pairs[p]
            if p % PAIRS == 0:
                o_ps = ps_o.tile([P, QTILES, DH], F32, name="o_ps", tag="o_ps")
                live[("o_ps", n, h)] = o_ps
            e_codes, e_scales = live[("e_codes", p)]
            for i in (i0, i0 + 1):
                for a in sides(n):
                    b, slot = (0, i - i0) if n == 0 else (i - i0, a)
                    nc.tensor.matmul_mx(
                        out=live[("o_ps", n, h)][:, i, :],
                        lhsT=e_codes[:, b, slot, :].bitcast(FP8X4),
                        lhsT_scale=e_scales[:, b, slot, :],
                        rhs=v_codes[:, n - 1 + a, h, :].bitcast(FP8X4),
                        rhs_scale=v_scales[:, n - 1 + a, h, :],
                        start=(a == sides(n)[0]),
                        stop=(a == OWN),
                    )

        def invert(g):
            recip = small.tile([P, 2 * QTILES], F32, name="recip", tag="recip")
            nc.vector.reciprocal(out=recip[:], in_=live[("sums", g // 2)][:])
            for k in range(2):
                live[("recip",) + groups[g - 1 + k]] = recip[:, k * QTILES : (k + 1) * QTILES]

        def put(n, h, first, end, o_sb):
            rows = slice(n * CHUNK + first * P, n * CHUNK + end * P)
            nc.sync.dma_start(
                out=out[0, rows, h * DH : (h + 1) * DH].rearrange("(i p) d -> p i d", p=P),
                in_=o_sb[:, first:end],
            )

        def finish(n, h, first=0, end=QTILES):
            o_sb = store.tile([P, QTILES, DH], F32, name="o_sb", tag="o_sb")
            tiles = slice(first, end)
            nc.vector.tensor_tensor(
                out=o_sb[:, tiles],
                in0=live[("o_ps", n, h)][:, tiles],
                in1=live[("recip", n, h)][:, tiles].unsqueeze(2).to_broadcast([P, end - first, DH]),
                op=ALU.mult,
            )
            put(n, h, first, end, o_sb)

        def finish_scalar(n, h, first=0, end=QTILES):
            o_sb = store.tile([P, QTILES, DH], F32, name="o_sb", tag="o_sb")
            for i in range(first, end):
                nc.scalar.activation(
                    out=o_sb[:, i, :], in_=live[("o_ps", n, h)][:, i, :], func=ACT.Copy, scale=live[("recip", n, h)][:, i : i + 1]
                )
            put(n, h, first, end, o_sb)

        load_qk(0, 0, 0, 2)
        load_qk(0, 0, 2, QTILES)
        load_wv(0, 0)
        load_wv(1, 0)
        load_hidden(0)
        load_qk(0, 1)
        load_wv(0, 1)
        load_wv(1, 1)
        load_hidden(1)
        load_qk(1, 0)
        load_qk(1, 1)

        extra = {}

        def at(step, place, fn, *args):
            extra.setdefault((step, place), []).append((fn, args))

        def run(step, place):
            for fn, args in extra.get((step, place), []):
                fn(*args)

        for g in range(HID_PASSES):
            for half, first in ((0, 3), (1, FIRST_VALUES)):
                at(first + g, "vector", wv_group, g, half)
                at(first + g + 1, "vector", wv_quantise, g, half)
        for n in range(CHUNKS):
            for t in range(QTILES):
                step = QTILES * n + t + 3
                at(step, "turn", hidden_turn, n, t)
                at(step + 1, "scalar", hidden_group, n, t)
                at(step + 2, "vector", hidden_quantise, n, t)
        v_step = []
        for g, (n, h) in enumerate(groups):
            step = max(PAIRS * g + 2, FIRST_VALUES + g)
            if g == len(groups) - 1:
                step -= 1
            v_step.append(step)
            at(step, "multiply", v_multiply, n, h)
            at(step, "scalar", v_group, n, h)
            at(step + 1, "vector", v_quantise, n, h)
            if g % 2:
                at(PAIRS * g + 4, "vector", invert, g)
            if g > 0:
                at(PAIRS * (g - 1), "turn", qk_turn, n, h)
                if g % 2:
                    at(PAIRS * (g - 1) + 1, "vector", qk_keep, n, h)
                else:
                    at(PAIRS * (g - 1) + 1, "scalar", qk_keep_scalar, n, h)

        count = len(pairs)
        done = 0
        with tc.manual_schedule():
            qk_turn(0, 0, 0, 2)
            qk_keep(0, 0, 0, 2)
            for step in range(count):
                if step == 6:
                    load_hidden(2)
                if step == PAIRS * HEADS:
                    load_qk(2, 0)
                    load_qk(2, 1)
                if 0 <= step - 1 < count:
                    row_max(step - 1)
                if step == 1:
                    qk_keep(0, 0, 2, QTILES)
                finished = None
                while done <= step - 6 and v_step[done // PAIRS] + 2 <= step and finished is None:
                    multiply(done)
                    done += 1
                    if done % PAIRS == 0:
                        finished = groups[done // PAIRS - 1]
                    if done == step - 5:
                        break
                run(step, "multiply")
                if step < count:
                    scores(step)
                if step == 0:
                    qk_turn(0, 0, 2, QTILES)
                if 0 <= step - 2 < count:
                    exponentials(step - 2)
                if 0 <= step - 3 < count:
                    regroup(step - 3)
                run(step, "scalar")
                if 0 <= step - 2 < count:
                    turn(step - 2)
                run(step, "vector")
                run(step, "turn")
                if finished:
                    finish(*finished)
                if 0 <= step - 4 < count:
                    quantise(step - 4)

            row_max(last)
            multiply(last - 5)
            multiply(last - 4)
            exponentials(last - 1)
            regroup(last - 2)
            turn(last - 1)
            exponentials(last)
            v_quantise(*groups[-1])
            regroup(last - 1)
            quantise(last - 3)
            turn(last)
            finish(*groups[-3])
            quantise(last - 2)
            multiply(last - 3)
            multiply(last - 2)
            regroup(last)
            invert(len(groups) - 1)
            quantise(last - 1)
            finish_scalar(*groups[-2])
            quantise(last)
            multiply(last - 1)
            multiply(last)
            finish_scalar(*groups[-1], 2, QTILES)
            finish(*groups[-1], 0, 2)
